import numpy as np
import ml_dtypes


def mxq(x, axis, fmt="e4m3"):
    dtype, down = {"e4m3": (ml_dtypes.float8_e4m3fn, 7), "e5m2": (ml_dtypes.float8_e5m2, 14)}[fmt]
    v = np.moveaxis(np.asarray(x, np.float32).astype(ml_dtypes.bfloat16).astype(np.float64), axis, -1)
    blocks = v.reshape(v.shape[:-1] + (-1, 32))
    amax = np.abs(blocks).max(-1, keepdims=True)
    byte = np.maximum(np.where(amax > 0, np.frexp(amax)[1] - 1 + 127, 0) - down, 1)
    scale = np.exp2(byte - 127.0)
    codes = (blocks / scale).astype(np.float32).astype(dtype).astype(np.float64)
    return np.moveaxis((codes * scale).reshape(v.shape), -1, axis)


WIDE = False


def mx_kscale(k):
    if not WIDE:
        return np.ones(k)
    levels = np.array([10, -10, 5, -5, 0])
    a = np.random.permutation(np.resize(levels, k // 512 * 4)).reshape(k // 512, 4)
    idx = np.arange(k)
    return np.exp2(a[idx // 512, idx % 128 // 32])


BF16 = ml_dtypes.bfloat16


def bf(x):
    return np.asarray(x, np.float32).astype(BF16)


def f64(x):
    return np.asarray(x).astype(np.float64)


B, H, W, D, Dh, Dq, R, T = 4, 16, 16, 1024, 1024, 128, 16, 8
EPS = 1e-6


def layer_norm(v, g, b):
    mu = v.mean(-1, keepdims=True)
    var = ((v - mu) ** 2).mean(-1, keepdims=True)
    return (v - mu) / np.sqrt(var + EPS) * g + b


def setup_inputs():
    rn = np.random.standard_normal
    s, t = mx_kscale(D), mx_kscale(Dh)
    return {
        "x": bf(rn((B, H, W, D)) * s),
        "z2": bf(rn((B, H, W, Dq)) * 1.5),
        "U1_w": bf(rn((Dh, D)) * np.sqrt(2.0 / D) / s),
        "U1_b": bf(rn(Dh) * 0.5),
        "U3_w": bf(rn((Dh, Dq)) * np.sqrt(2.0 / Dq)),
        "U3_b": bf(rn(Dh) * 0.5),
        "C_w": bf(rn((D, Dh)) / np.sqrt(Dh) / t),
        "C_b": bf(rn(D) * 0.3),
        "ln1_g": bf((1.0 + 0.1 * rn(Dh)) * t),
        "ln1_b": bf(0.2 * rn(Dh) * t),
        "ln3_g": bf(1.0 + 0.1 * rn(Dh)),
        "ln3_b": bf(0.2 * rn(Dh)),
        "alpha": bf(0.6 + 0.2 * np.random.random(1)),
    }


def reference(x, z2, U1_w, U1_b, U3_w, U3_b, C_w, C_b, ln1_g, ln1_b, ln3_g, ln3_b, alpha):
    out1 = (mxq(f64(x), 3, "e4m3") @ mxq(f64(U1_w), 1, "e4m3").T) + f64(U1_b)
    out3 = f64(z2) @ f64(U3_w).T + f64(U3_b)
    o1 = layer_norm(out1, f64(ln1_g), f64(ln1_b))
    o3 = layer_norm(out3, f64(ln3_g), f64(ln3_b))
    h = o1 + f64(alpha) * (o1 * o3)
    return (mxq(h, 3, "e4m3") @ mxq(f64(C_w), 1, "e4m3").T) + f64(C_b)

@@ -1,0 +1,314 @@
+from contextlib import ExitStack
+
+import concourse.mybir as mybir
+from concourse.masks import make_identity
+
+F32 = mybir.dt.float32
+BF16 = mybir.dt.bfloat16
+U32 = mybir.dt.uint32
+U8 = mybir.dt.uint8
+FP8X4 = mybir.dt.float8_e4m3fn_x4
+ALU = mybir.AluOpType
+ACT = mybir.ActivationFunctionType
+
+P = 128
+NT = 8
+D = 1024
+EPS = 1e-6
+FLOPS = 2 * 1024 * (1024 * 1024 * 2 + 128 * 1024)
+
+
+def tile_polymlp_skiplora_pa_kernel(
+    tc, x, z2, U1_w, U1_b, U3_w, U3_b, C_w, C_b, ln1_g, ln1_b, ln3_g, ln3_b, alpha, out
+):
+    nc = tc.nc
+    with ExitStack() as ctx:
+        const = ctx.enter_context(tc.tile_pool(name="const", bufs=1))
+        rawp = ctx.enter_context(tc.tile_pool(name="rawp", bufs=6))
+        browp = ctx.enter_context(tc.tile_pool(name="browp", bufs=2))
+        grp = ctx.enter_context(tc.tile_pool(name="grp", bufs=2))
+        vnp = ctx.enter_context(tc.tile_pool(name="vnp", bufs=1))
+        stat = ctx.enter_context(tc.tile_pool(name="stat", bufs=4))
+        junkp = ctx.enter_context(tc.tile_pool(name="junkp", bufs=1))
+        op = ctx.enter_context(tc.tile_pool(name="op", bufs=2))
+        otp = ctx.enter_context(tc.tile_pool(name="otp", bufs=2))
+        pmm = ctx.enter_context(tc.psum_pool(name="pmm", bufs=4))
+        ptp = ctx.enter_context(tc.psum_pool(name="ptp", bufs=4))
+
+        xf = x.flatten_outer_dims()
+        zf = z2.flatten_outer_dims()
+        of = out.flatten_outer_dims()
+        x_v = xf.rearrange("(p c j) d -> c p (j d)", c=4, j=2)
+        z_v = zf.rearrange("(p i) q -> p (i q)", i=NT)
+        o_v = of.rearrange("(p i) d -> p i d", i=NT)
+        u1_v = U1_w.rearrange("(a p e) d -> a p (e d)", a=4, e=2)
+        u3_v = U3_w.rearrange("(a p e) q -> p a (e q)", a=4, e=2)
+        c_v = C_w.rearrange("(c j p) h -> c p j h", c=4, j=2)
+
+        identB = const.tile([P, P], BF16)
+        make_identity(nc, identB[:])
+        identF = const.tile([P, P], F32)
+        make_identity(nc, identF[:])
+        ones = const.tile([P, P], BF16)
+        nc.vector.memset(ones[:], 1.0)
+        mhalf = const.tile([P, 1], F32)
+        nc.vector.memset(mhalf[:], -0.5)
+        vrows = const.tile([P, P], F32)
+        nc.vector.memset(vrows[:], 0.0)
+
+        def bias_row(vec):
+            brow = browp.tile([P, D], BF16, tag="brow", name="brow")
+            nc.vector.memset(brow[:], 0.0)
+            nc.sync.dma_start(out=brow[0:1, :], in_=vec.rearrange("(o n) -> o n", o=1))
+            return brow
+
+        def load_raw(src, nm, split):
+            t = rawp.tile([P, 2 * D], BF16, tag="raw", name=nm)
+            if split:
+                nc.sync.dma_start(out=t[:].rearrange("p (j h) -> p j h", j=2), in_=src)
+            else:
+                nc.sync.dma_start(out=t[:], in_=src)
+            return t
+
+        brow3 = bias_row(U3_b)
+        z2raw = const.tile([P, D], BF16)
+        nc.sync.dma_start(out=z2raw[:], in_=z_v)
+        u3raw = const.tile([P, D], BF16)
+        nc.sync.dma_start(out=u3raw[:].rearrange("p (a w) -> p a w", a=4), in_=u3_v)
+        u1raw = [load_raw(u1_v[a], "u1raw%d" % a, False) for a in range(4)]
+        brow1 = bias_row(U1_b)
+        xraw = [load_raw(x_v[c], "xraw%d" % c, False) for c in range(2)]
+
+        xq = const.tile([P, 2048], U32, align_bytes=64)
+        xs = const.tile([P, 2048], U8, align_bytes=64)
+        u1q = const.tile([P, 2048], U32, align_bytes=64)
+        u1s = const.tile([P, 2048], U8, align_bytes=64)
+        cq = const.tile([P, 2048], U32, align_bytes=64)
+        cs = const.tile([P, 2048], U8, align_bytes=64)
+        hq = const.tile([P, 2048], U32, align_bytes=64)
+        hs = const.tile([P, 2048], U8, align_bytes=64)
+
+        def word_transposes(raw, half):
+            bank = ptp.tile([P, 512], F32, tag="tp", name="wbank")
+            words = raw[:].bitcast(F32)
+            for c in range(4):
+                nc.tensor.transpose(
+                    out=bank[:, c * P : (c + 1) * P],
+                    in_=words[:, half * 512 + c * P : half * 512 + (c + 1) * P],
+                    identity=identF[:],
+                )
+            return bank
+
+        def prep_weight(raws, codes, scales, engines):
+            for hf in range(2):
+                wg = grp.tile([P, 4096], BF16, tag="wg", name="wg", align_bytes=64)
+                wgv = wg[:].bitcast(F32).rearrange("p (g j r u) -> p g j r u", g=2, j=4, u=2)
+                for jl in range(4):
+                    jt = 4 * hf + jl
+                    bank = word_transposes(raws[jt // 2], jt % 2)
+                    src = bank[:].rearrange("p (g u r) -> p g r u", g=2, u=2)
+                    if engines[jt % len(engines)] == "act":
+                        nc.scalar.copy(out=wgv[:, :, jl, :, :], in_=src)
+                    else:
+                        nc.vector.tensor_copy(out=wgv[:, :, jl, :, :], in_=src)
+                for g in range(2):
+                    sl = slice(g * 1024 + hf * 512, g * 1024 + hf * 512 + 512)
+                    nc.vector.quantize_mx(
+                        out=codes[:, sl].bitcast(FP8X4),
+                        scales=scales[:, sl],
+                        in_=wg[:, g * 2048 : (g + 1) * 2048],
+                    )
+
+        def prep_x(c):
+            xg = grp.tile([P, 2048], BF16, tag="xg", name="xg", align_bytes=64)
+            xgv = xg[:].bitcast(F32).rearrange("p (j g r u) -> p j g r u", j=2, g=2, u=2)
+            for j in range(2):
+                bank = word_transposes(xraw[c], j)
+                nc.scalar.copy(
+                    out=xgv[:, j, :, :, :],
+                    in_=bank[:].rearrange("p (g u r) -> p g r u", g=2, u=2),
+                )
+            sl = slice(c * 512, (c + 1) * 512)
+            nc.vector.quantize_mx(out=xq[:, sl].bitcast(FP8X4), scales=xs[:, sl], in_=xg[:])
+
+        def bias_plane(brow, nm, permute):
+            bc = const.tile([P, D], F32, name=nm)
+            for hf in range(2):
+                ps = pmm.tile([P, 512], F32, tag="mm", name="bps")
+                nc.tensor.matmul(
+                    out=ps[:], lhsT=ones[:], rhs=brow[:, hf * 512 : (hf + 1) * 512], start=True, stop=True
+                )
+                dst = bc[:, hf * 512 : (hf + 1) * 512]
+                if permute:
+                    nc.vector.tensor_copy(
+                        out=dst.rearrange("p (a e r) -> p a e r", a=2, e=2),
+                        in_=ps[:].rearrange("p (a r e) -> p a e r", a=2, e=2),
+                    )
+                else:
+                    nc.vector.tensor_copy(out=dst, in_=ps[:])
+            return bc
+
+        def norm_unit(nm_, ps_pair, bc):
+            v = vnp.tile([P, D], F32, name=nm_)
+            ssum = stat.tile([P, 2], F32, tag="ssum", name="ssum")
+            for hf in range(2):
+                sl = slice(hf * 512, (hf + 1) * 512)
+                nc.vector.scalar_tensor_tensor(
+                    out=v[:, sl], in0=ps_pair[hf][:], scalar=1.0, in1=bc[:, sl],
+                    op0=ALU.mult, op1=ALU.add, accum_out=ssum[:, hf : hf + 1],
+                )
+            negmean = stat.tile([P, 1], F32, tag="negmean", name="negmean")
+            nc.gpsimd.tensor_scalar(
+                out=negmean[:], in0=ssum[:, 0:1], scalar1=ssum[:, 1:2], scalar2=-1.0 / D,
+                op0=ALU.add, op1=ALU.mult,
+            )
+            junk = junkp.tile([P, D], BF16, tag="junk", name="junk")
+            sq = stat.tile([P, 1], F32, tag="sq", name="sq")
+            nc.scalar.activation(
+                out=junk[:], in_=v[:], func=ACT.Square, bias=negmean[:, 0:1], scale=1.0, accum_out=sq[:, 0:1]
+            )
+            vare = stat.tile([P, 1], F32, tag="vare", name="vare")
+            nc.gpsimd.tensor_scalar(
+                out=vare[:], in0=sq[:], scalar1=1.0 / D, scalar2=EPS, op0=ALU.mult, op1=ALU.add
+            )
+            rstd = stat.tile([P, 1], F32, tag="rstd", name="rstd")
+            nc.gpsimd.tensor_tensor(out=rstd[:], in0=vare[:], in1=mhalf[:], op=ALU.pow)
+            nc.gpsimd.tensor_scalar(
+                out=v[:], in0=v[:], scalar1=negmean[:, 0:1], scalar2=rstd[:, 0:1], op0=ALU.add, op1=ALU.mult
+            )
+            return v
+
+        def branch3(i):
+            pair = []
+            for hf in range(2):
+                ps = pmm.tile([P, 512], F32, tag="mm", name="ps3")
+                nc.tensor.matmul(
+                    out=ps[:], lhsT=z2T[:, i * P : (i + 1) * P], rhs=u3T[:, hf * 512 : (hf + 1) * 512],
+                    start=True, stop=True,
+                )
+                pair.append(ps)
+            return norm_unit("n3_%d" % i, pair, bc3)
+
+        def branch1(i):
+            pair = []
+            for hf in range(2):
+                ps = pmm.tile([P, 512], F32, tag="mm", name="ps1")
+                for g in range(2):
+                    ls = slice(i * 256 + g * P, i * 256 + (g + 1) * P)
+                    rs = slice(g * 1024 + hf * 512, g * 1024 + hf * 512 + 512)
+                    nc.tensor.matmul_mx(
+                        out=ps[:], lhsT=xq[:, ls].bitcast(FP8X4), lhsT_scale=xs[:, ls],
+                        rhs=u1q[:, rs].bitcast(FP8X4), rhs_scale=u1s[:, rs],
+                        start=(g == 0), stop=(g == 1),
+                    )
+                pair.append(ps)
+            return norm_unit("n1_%d" % i, pair, bc1)
+
+        def gate_group(grp_i):
+            for g in range(2):
+                o1 = op.tile([P, 4, 512], F32, tag="o1", name="o1")
+                o3 = op.tile([P, 4, 512], F32, tag="o3", name="o3")
+                for t in range(4):
+                    jt = 4 * g + t
+                    for (ns, dst, gcol, bcol) in (
+                        (n1, o1, cols[:, jt : jt + 1], cols[:, 8 + jt : 9 + jt]),
+                        (n3, o3, g3p[:, jt : jt + 1], b3p[:, jt : jt + 1]),
+                    ):
+                        bank = ptp.tile([P, 512], F32, tag="tp", name="nbank")
+                        for il in range(4):
+                            nc.tensor.transpose(
+                                out=bank[:, il * P : (il + 1) * P],
+                                in_=ns[4 * grp_i + il][:, jt * P : (jt + 1) * P],
+                                identity=identF[:],
+                            )
+                        nc.scalar.activation(
+                            out=dst[:, t, :], in_=bank[:], func=ACT.Identity, bias=bcol, scale=gcol
+                        )
+                hg = grp.tile([P, 2048], BF16, tag="hg", name="hg", align_bytes=64)
+                nc.vector.tensor_tensor(
+                    out=hg[:].rearrange("p (c i t) -> p c t i", i=4, t=4),
+                    in0=o1[:].rearrange("p t (c i) -> p c t i", i=4),
+                    in1=o3[:].rearrange("p t (c i) -> p c t i", i=4),
+                    op=ALU.mult,
+                )
+                sl = slice(g * 1024 + grp_i * 512, g * 1024 + grp_i * 512 + 512)
+                nc.vector.quantize_mx(out=hq[:, sl].bitcast(FP8X4), scales=hs[:, sl], in_=hg[:])
+
+        def stage2(i):
+            ot = otp.tile([P, D], F32, tag="ot", name="ot")
+            for hf in range(2):
+                ps = pmm.tile([P, 512], F32, tag="mm", name="ps2")
+                for g in range(2):
+                    ls = slice(g * 1024 + i * P, g * 1024 + (i + 1) * P)
+                    rs = slice(g * 1024 + hf * 512, g * 1024 + hf * 512 + 512)
+                    nc.tensor.matmul_mx(
+                        out=ps[:], lhsT=hq[:, ls].bitcast(FP8X4), lhsT_scale=hs[:, ls],
+                        rhs=cq[:, rs].bitcast(FP8X4), rhs_scale=cs[:, rs],
+                        start=(g == 0), stop=(g == 1),
+                    )
+                sl = slice(hf * 512, (hf + 1) * 512)
+                nc.vector.tensor_tensor(out=ot[:, sl], in0=ps[:], in1=bcc[:, sl], op=ALU.add)
+            nc.sync.dma_start(out=o_v[:, i, :], in_=ot[:])
+
+        z2T = const.tile([P, D], BF16)
+        u3T = const.tile([P, D], BF16)
+        for (raw, dstT) in ((z2raw, z2T), (u3raw, u3T)):
+            pb = ptp.tile([P, D], BF16, tag="tp", name="pb")
+            for k in range(8):
+                nc.tensor.transpose(
+                    out=pb[:, k * P : (k + 1) * P], in_=raw[:, k * P : (k + 1) * P], identity=identB[:]
+                )
+            nc.scalar.copy(out=dstT[:], in_=pb[:])
+        bc3 = bias_plane(brow3, "bc3", True)
+        n1 = []
+        n3 = []
+        for i in range(4):
+            n3.append(branch3(i))
+        prep_weight(u1raw, u1q, u1s, ("act", "dve"))
+        bc1 = bias_plane(brow1, "bc1", True)
+        xraw.append(load_raw(x_v[2], "xraw2", False))
+        xraw.append(load_raw(x_v[3], "xraw3", False))
+        for v, vec in enumerate((ln1_g, ln1_b, ln3_g, ln3_b)):
+            nc.sync.dma_start(
+                out=vrows[4 * v : 4 * v + 4, :].bitcast(BF16), in_=vec.rearrange("(r w) -> r w", r=4)
+            )
+        al_bf = const.tile([P, 1], BF16)
+        nc.sync.dma_start(out=al_bf[:], in_=alpha.partition_broadcast(P))
+        browc = bias_row(C_b)
+        craw = [load_raw(c_v[c], "craw%d" % c, True) for c in range(2)]
+        prep_x(0)
+        prep_x(1)
+        craw.append(load_raw(c_v[2], "craw2", True))
+        craw.append(load_raw(c_v[3], "craw3", True))
+        for i in range(4):
+            n1.append(branch1(i))
+        pv = ptp.tile([P, 512], F32, tag="tp", name="pv")
+        nc.tensor.transpose(out=pv[:, 0:P], in_=vrows[:], identity=identF[:])
+        vw = const.tile([P, 16], F32)
+        nc.vector.tensor_copy(out=vw[:], in_=pv[:, 0:16])
+        cols = const.tile([P, 32], F32)
+        nc.vector.tensor_copy(out=cols[:], in_=vw[:].bitcast(BF16))
+        al = const.tile([P, 1], F32)
+        nc.vector.tensor_copy(out=al[:], in_=al_bf[:])
+        g3p = const.tile([P, 8], F32)
+        nc.vector.tensor_scalar(
+            out=g3p[:], in0=cols[:, 16:24], scalar1=al[:, 0:1], scalar2=None, op0=ALU.mult
+        )
+        b3p = const.tile([P, 8], F32)
+        nc.vector.tensor_scalar(
+            out=b3p[:], in0=cols[:, 24:32], scalar1=al[:, 0:1], scalar2=1.0, op0=ALU.mult, op1=ALU.add
+        )
+        prep_x(2)
+        prep_x(3)
+        for i in range(4, 8):
+            n3.append(branch3(i))
+        prep_weight(craw, cq, cs, ("act",))
+        bcc = bias_plane(browc, "bcc", False)
+        for i in range(4, 8):
+            n1.append(branch1(i))
+        gate_group(0)
+        for i in range(4):
+            stage2(i)
+        gate_group(1)
+        for i in range(4, 8):
+            stage2(i)

@@ -16,6 +16,46 @@ NT = 8
 D = 1024
 EPS = 1e-6
 FLOPS = 2 * 1024 * (1024 * 1024 * 2 + 128 * 1024)
+PINNED = True
+PROGRAM = (
+    ('ZU', 0), ('BC', 3), ('ZU', 1), ('A', 3, 0, 'pool'), ('A', 3, 1, 'pool'), ('W', 'U', 0, 'act'),
+    ('W', 'U', 1, 'dve'), ('A', 3, 2, 'pool'), ('W', 'U', 2, 'act'), ('W', 'U', 3, 'dve'), ('WQ', 'U', 0), ('A', 3, 3, 'pool'),
+    ('W', 'U', 4, 'act'), ('W', 'U', 5, 'dve'), ('W', 'U', 6, 'act'), ('W', 'U', 7, 'dve'), ('WQ', 'U', 1), ('BC', 1),
+    ('X', 0, 'act'), ('X', 1, 'act'), ('XQ', 0), ('A', 1, 0, 'pool'), ('A', 1, 1, 'pool'), ('X', 2, 'act'),
+    ('X', 3, 'act'), ('XQ', 1), ('COLS',), ('A', 1, 2, 'pool'), ('A', 1, 3, 'pool'), ('X', 4, 'act'),
+    ('X', 5, 'act'), ('XQ', 2), ('X', 6, 'act'), ('X', 7, 'act'), ('XQ', 3), ('B', 0, 2, 0, 0, 'act'),
+    ('B', 0, 2, 0, 1, 'act'), ('B', 0, 2, 0, 2, 'act'), ('B', 0, 2, 0, 3, 'act'), ('F', 0, 2, 0), ('B', 0, 2, 1, 0, 'act'), ('B', 0, 2, 1, 1, 'act'),
+    ('B', 0, 2, 1, 2, 'act'), ('B', 0, 2, 1, 3, 'act'), ('F', 0, 2, 1), ('A', 3, 4, 'pool'), ('A', 3, 5, 'pool'), ('W', 'C', 0, 'act'),
+    ('W', 'C', 1, 'act'), ('W', 'C', 2, 'act'), ('W', 'C', 3, 'act'), ('WQ', 'C', 0), ('W', 'C', 4, 'act'), ('W', 'C', 5, 'act'),
+    ('W', 'C', 6, 'act'), ('W', 'C', 7, 'act'), ('WQ', 'C', 1), ('A', 1, 4, 'pool'), ('A', 1, 5, 'pool'), ('B', 2, 2, 0, 0, 'act'),
+    ('B', 2, 2, 0, 1, 'act'), ('B', 2, 2, 0, 2, 'act'), ('B', 2, 2, 0, 3, 'act'), ('F', 2, 2, 0), ('B', 2, 2, 1, 0, 'act'), ('B', 2, 2, 1, 1, 'act'),
+    ('B', 2, 2, 1, 2, 'act'), ('B', 2, 2, 1, 3, 'act'), ('F', 2, 2, 1), ('S', 0), ('S', 1), ('A', 3, 6, 'pool'),
+    ('A', 3, 7, 'pool'), ('A', 1, 6, 'pool'), ('A', 1, 7, 'pool'), ('S', 2), ('S', 3), ('B', 4, 2, 0, 0, 'act'),
+    ('B', 4, 2, 0, 1, 'act'), ('B', 4, 2, 0, 2, 'act'), ('B', 4, 2, 0, 3, 'act'), ('F', 4, 2, 0), ('B', 4, 2, 1, 0, 'act'), ('B', 4, 2, 1, 1, 'act'),
+    ('B', 4, 2, 1, 2, 'act'), ('B', 4, 2, 1, 3, 'act'), ('F', 4, 2, 1), ('S', 4), ('S', 5), ('B', 6, 2, 0, 0, 'act'),
+    ('B', 6, 2, 0, 1, 'act'), ('B', 6, 2, 0, 2, 'act'), ('B', 6, 2, 0, 3, 'act'), ('F', 6, 2, 0), ('B', 6, 2, 1, 0, 'act'), ('B', 6, 2, 1, 1, 'act'),
+    ('B', 6, 2, 1, 2, 'act'), ('B', 6, 2, 1, 3, 'act'), ('F', 6, 2, 1), ('S', 6), ('S', 7),
+)
+LAGS = {'ZU': (0, 0, 0, 0, 0, 0, 0, 0), 'BC': (0, 0, 0, 0, 0, 0, 0, 0), 'W': (0, 0, 0, 0, 0, 0, 0, 0), 'WQ': (0, 0, 0, 0, 0, 0, 0, 0), 'X': (0, 0, 0, 0, 0, 0, 0, 0), 'XQ': (0, 0, 0, 0, 0, 0, 0, 0), 'A': (0, 0, 0, 0, 0, 0, 0, 0), 'COLS': (0, 0, 0, 0, 0, 0, 0, 0), 'B': (0, 0, 0, 0, 0, 0, 0, 0), 'F': (0, 0, 0, 0, 0, 0, 0, 0), 'S': (0, 0, 0, 0, 0, 0, 0, 0)}
+ORDER = (
+    0, 2, 4, 1, 6, 3, 5, 8, 16, 7, 24, 9, 10, 17, 18, 26, 11, 25, 28, 19, 30, 12, 13, 36,
+    27, 20, 38, 29, 42, 21, 14, 44, 31, 50, 15, 39, 52, 37, 43, 54, 51, 40, 56, 22, 55, 41, 60, 23,
+    62, 45, 64, 53, 66, 65, 57, 85, 32, 67, 46, 58, 87, 33, 59, 90, 108, 61, 154, 47, 63, 156, 34, 162,
+    68, 35, 164, 91, 86, 110, 155, 88, 113, 157, 109, 69, 48, 89, 111, 71, 49, 70, 115, 72, 114, 77, 112, 79,
+    73, 158, 74, 78, 118, 122, 80, 92, 116, 75, 163, 94, 119, 76, 93, 123, 100, 159, 95, 126, 102, 101, 130, 81,
+    96, 82, 160, 136, 103, 140, 161, 190, 117, 192, 97, 165, 198, 191, 83, 200, 127, 193, 131, 84, 144, 137, 199, 148,
+    141, 170, 145, 201, 149, 172, 171, 98, 174, 120, 173, 124, 99, 121, 128, 125, 132, 138, 129, 133, 142, 139, 134, 104,
+    146, 166, 175, 194, 150, 202, 252, 105, 176, 135, 253, 254, 260, 143, 262, 255, 106, 268, 147, 180, 151, 107, 261, 167,
+    182, 152, 184, 177, 168, 153, 270, 181, 263, 186, 169, 183, 178, 206, 185, 179, 208, 187, 276, 269, 210, 256, 264, 195,
+    242, 188, 212, 189, 247, 203, 196, 243, 197, 248, 244, 207, 271, 249, 209, 214, 211, 245, 216, 213, 218, 215, 204, 277,
+    246, 220, 217, 224, 219, 205, 226, 221, 228, 225, 222, 230, 227, 232, 229, 234, 231, 236, 272, 223, 233, 238, 235, 237,
+    278, 239, 250, 257, 294, 240, 296, 251, 298, 300, 265, 258, 241, 279, 284, 259, 286, 273, 285, 289, 287, 291, 266, 295,
+    290, 297, 288, 302, 267, 299, 304, 292, 301, 306, 303, 308, 293, 305, 312, 307, 314, 309, 316, 274, 313, 310, 318, 315,
+    320, 275, 317, 322, 319, 324, 311, 321, 326, 323, 340, 325, 344, 327, 348, 280, 341, 328, 352, 281, 358, 329, 345, 330,
+    282, 349, 353, 332, 283, 359, 331, 335, 333, 337, 336, 334, 362, 342, 338, 346, 363, 350, 343, 339, 354, 347, 360, 351,
+    364, 355, 366, 361, 356, 368, 365, 370, 367, 372, 369, 357, 371, 373, 374, 375, 376, 378, 377, 381, 379, 383, 382, 380,
+    384, 385,
+)
 
 
 def tile_polymlp_skiplora_pa_kernel(
@@ -24,7 +64,7 @@ def tile_polymlp_skiplora_pa_kernel(
     nc = tc.nc
     with ExitStack() as ctx:
         const = ctx.enter_context(tc.tile_pool(name="const", bufs=1))
-        rawp = ctx.enter_context(tc.tile_pool(name="rawp", bufs=6))
+        rawp = ctx.enter_context(tc.tile_pool(name="rawp", bufs=12))
         browp = ctx.enter_context(tc.tile_pool(name="browp", bufs=2))
         grp = ctx.enter_context(tc.tile_pool(name="grp", bufs=2))
         vnp = ctx.enter_context(tc.tile_pool(name="vnp", bufs=1))
@@ -34,6 +74,8 @@ def tile_polymlp_skiplora_pa_kernel(
         otp = ctx.enter_context(tc.tile_pool(name="otp", bufs=2))
         pmm = ctx.enter_context(tc.psum_pool(name="pmm", bufs=4))
         ptp = ctx.enter_context(tc.psum_pool(name="ptp", bufs=4))
+        if PINNED:
+            ctx.enter_context(tc.manual_schedule())
 
         xf = x.flatten_outer_dims()
         zf = z2.flatten_outer_dims()
@@ -45,19 +87,20 @@ def tile_polymlp_skiplora_pa_kernel(
         u3_v = U3_w.rearrange("(a p e) q -> p a (e q)", a=4, e=2)
         c_v = C_w.rearrange("(c j p) h -> c p j h", c=4, j=2)
 
+        u3raw = const.tile([P, D], BF16)
+        nc.sync.dma_start(out=u3raw[:].rearrange("p (a w) -> p a w", a=4), in_=u3_v)
+        z2raw = const.tile([P, D], BF16)
+        nc.sync.dma_start(out=z2raw[:], in_=z_v)
+
         identB = const.tile([P, P], BF16)
         make_identity(nc, identB[:])
         identF = const.tile([P, P], F32)
         make_identity(nc, identF[:])
         ones = const.tile([P, P], BF16)
         nc.vector.memset(ones[:], 1.0)
-        mhalf = const.tile([P, 1], F32)
-        nc.vector.memset(mhalf[:], -0.5)
-        vrows = const.tile([P, P], F32)
-        nc.vector.memset(vrows[:], 0.0)
 
-        def bias_row(vec):
-            brow = browp.tile([P, D], BF16, tag="brow", name="brow")
+        def bias_row(vec, nm):
+            brow = browp.tile([P, D], BF16, tag="brow", name=nm)
             nc.vector.memset(brow[:], 0.0)
             nc.sync.dma_start(out=brow[0:1, :], in_=vec.rearrange("(o n) -> o n", o=1))
             return brow
@@ -70,14 +113,23 @@ def tile_polymlp_skiplora_pa_kernel(
                 nc.sync.dma_start(out=t[:], in_=src)
             return t
 
-        brow3 = bias_row(U3_b)
-        z2raw = const.tile([P, D], BF16)
-        nc.sync.dma_start(out=z2raw[:], in_=z_v)
-        u3raw = const.tile([P, D], BF16)
-        nc.sync.dma_start(out=u3raw[:].rearrange("p (a w) -> p a w", a=4), in_=u3_v)
+        brows = {3: bias_row(U3_b, "brow3")}
+        mhalf = const.tile([P, 1], F32)
+        nc.vector.memset(mhalf[:], -0.5)
+        vrows = const.tile([P, P], F32)
+        nc.vector.memset(vrows[:], 0.0)
         u1raw = [load_raw(u1_v[a], "u1raw%d" % a, False) for a in range(4)]
-        brow1 = bias_row(U1_b)
-        xraw = [load_raw(x_v[c], "xraw%d" % c, False) for c in range(2)]
+        brows[1] = bias_row(U1_b, "brow1")
+        xraw = [load_raw(x_v[c], "xraw%d" % c, False) for c in range(4)]
+        for v, vec in enumerate((ln1_g, ln1_b, ln3_g, ln3_b)):
+            nc.sync.dma_start(
+                out=vrows[4 * v : 4 * v + 4, :].bitcast(BF16), in_=vec.rearrange("(r w) -> r w", r=4)
+            )
+        al_bf = const.tile([P, 1], BF16)
+        nc.sync.dma_start(out=al_bf[:], in_=alpha.partition_broadcast(P))
+        craw = [load_raw(c_v[c], "craw%d" % c, True) for c in range(4)]
+        bcc = const.tile([P, D], BF16)
+        nc.sync.dma_start(out=bcc[:], in_=C_b.partition_broadcast(P))
 
         xq = const.tile([P, 2048], U32, align_bytes=64)
         xs = const.tile([P, 2048], U8, align_bytes=64)
@@ -87,9 +139,21 @@ def tile_polymlp_skiplora_pa_kernel(
         cs = const.tile([P, 2048], U8, align_bytes=64)
         hq = const.tile([P, 2048], U32, align_bytes=64)
         hs = const.tile([P, 2048], U8, align_bytes=64)
+        zuT = const.tile([P, 2048], BF16)
+        bcs = {1: const.tile([P, D], F32, name="bc1"), 3: const.tile([P, D], F32, name="bc3")}
+        cols = const.tile([P, 32], F32)
+        g3p = const.tile([P, 8], F32)
+        b3p = const.tile([P, 8], F32)
+        wsrc = {"U": (u1raw, u1q, u1s), "C": (craw, cq, cs)}
 
-        def word_transposes(raw, half):
-            bank = ptp.tile([P, 512], F32, tag="tp", name="wbank")
+        ops = []
+        live = {}
+
+        def at(pos, lag, fn):
+            ops.append((pos + lag, len(ops), fn))
+
+        def word_transposes(raw, half, nm):
+            bank = ptp.tile([P, 512], F32, tag="tp", name=nm)
             words = raw[:].bitcast(F32)
             for c in range(4):
                 nc.tensor.transpose(
@@ -99,145 +163,261 @@ def tile_polymlp_skiplora_pa_kernel(
                 )
             return bank
 
-        def prep_weight(raws, codes, scales, engines):
-            for hf in range(2):
-                wg = grp.tile([P, 4096], BF16, tag="wg", name="wg", align_bytes=64)
-                wgv = wg[:].bitcast(F32).rearrange("p (g j r u) -> p g j r u", g=2, j=4, u=2)
-                for jl in range(4):
-                    jt = 4 * hf + jl
-                    bank = word_transposes(raws[jt // 2], jt % 2)
-                    src = bank[:].rearrange("p (g u r) -> p g r u", g=2, u=2)
-                    if engines[jt % len(engines)] == "act":
-                        nc.scalar.copy(out=wgv[:, :, jl, :, :], in_=src)
-                    else:
-                        nc.vector.tensor_copy(out=wgv[:, :, jl, :, :], in_=src)
-                for g in range(2):
-                    sl = slice(g * 1024 + hf * 512, g * 1024 + hf * 512 + 512)
-                    nc.vector.quantize_mx(
-                        out=codes[:, sl].bitcast(FP8X4),
-                        scales=scales[:, sl],
-                        in_=wg[:, g * 2048 : (g + 1) * 2048],
+        def copy_on(engine, dst, src):
+            if engine == "act":
+                nc.scalar.copy(out=dst, in_=src)
+            else:
+                nc.vector.tensor_copy(out=dst, in_=src)
+
+        def unit_zu(pos, k):
+            lag = LAGS["ZU"]
+
+            def pe():
+                pb = ptp.tile([P, D], BF16, tag="tp", name="pb%d" % k)
+                live["pb", k] = pb
+                for m in range(8):
+                    raw = u3raw if m < 4 else z2raw
+                    col = (4 * k + m % 4) * P
+                    nc.tensor.transpose(
+                        out=pb[:, m * P : (m + 1) * P], in_=raw[:, col : col + P], identity=identB[:]
                     )
 
-        def prep_x(c):
-            xg = grp.tile([P, 2048], BF16, tag="xg", name="xg", align_bytes=64)
-            xgv = xg[:].bitcast(F32).rearrange("p (j g r u) -> p j g r u", j=2, g=2, u=2)
-            for j in range(2):
-                bank = word_transposes(xraw[c], j)
-                nc.scalar.copy(
-                    out=xgv[:, j, :, :, :],
-                    in_=bank[:].rearrange("p (g u r) -> p g r u", g=2, u=2),
-                )
-            sl = slice(c * 512, (c + 1) * 512)
-            nc.vector.quantize_mx(out=xq[:, sl].bitcast(FP8X4), scales=xs[:, sl], in_=xg[:])
+            def ev():
+                nc.scalar.copy(out=zuT[:, k * D : (k + 1) * D], in_=live["pb", k][:])
 
-        def bias_plane(brow, nm, permute):
-            bc = const.tile([P, D], F32, name=nm)
-            for hf in range(2):
-                ps = pmm.tile([P, 512], F32, tag="mm", name="bps")
+            at(pos, lag[0], pe)
+            at(pos, lag[1], ev)
+
+        def unit_bc(pos, br):
+            lag = LAGS["BC"]
+
+            def pe(hf):
+                ps = pmm.tile([P, 512], F32, tag="mm", name="bps%d%d" % (br, hf))
+                live["bps", br, hf] = ps
                 nc.tensor.matmul(
-                    out=ps[:], lhsT=ones[:], rhs=brow[:, hf * 512 : (hf + 1) * 512], start=True, stop=True
+                    out=ps[:], lhsT=ones[:], rhs=brows[br][:, hf * 512 : (hf + 1) * 512], start=True, stop=True
                 )
-                dst = bc[:, hf * 512 : (hf + 1) * 512]
-                if permute:
-                    nc.vector.tensor_copy(
-                        out=dst.rearrange("p (a e r) -> p a e r", a=2, e=2),
-                        in_=ps[:].rearrange("p (a r e) -> p a e r", a=2, e=2),
+
+            def ev(hf):
+                nc.vector.tensor_copy(
+                    out=bcs[br][:, hf * 512 : (hf + 1) * 512].rearrange("p (a e r) -> p a e r", a=2, e=2),
+                    in_=live["bps", br, hf][:].rearrange("p (a r e) -> p a e r", a=2, e=2),
+                )
+
+            for hf in range(2):
+                at(pos, lag[0], lambda hf=hf: pe(hf))
+                at(pos, lag[1], lambda hf=hf: ev(hf))
+
+        def unit_w(pos, w, jt, engine):
+            lag = LAGS["W"]
+            hf = jt // 4
+
+            def pe():
+                live["wb", w, jt] = word_transposes(wsrc[w][0][jt // 2], jt % 2, "wb%s%d" % (w, jt))
+
+            def ev():
+                if ("wg", w, hf) not in live:
+                    live["wg", w, hf] = grp.tile([P, 4096], BF16, tag="wg", name="wg%s%d" % (w, hf), align_bytes=64)
+                wgv = live["wg", w, hf][:].bitcast(F32).rearrange("p (g j r u) -> p g j r u", g=2, j=4, u=2)
+                copy_on(
+                    engine, wgv[:, :, jt % 4, :, :],
+                    live["wb", w, jt][:].rearrange("p (g u r) -> p g r u", g=2, u=2),
+                )
+
+            at(pos, lag[0], pe)
+            at(pos, lag[1], ev)
+
+        def unit_wq(pos, w, hf):
+            def qz(g):
+                sl = slice(g * 1024 + hf * 512, g * 1024 + hf * 512 + 512)
+                nc.vector.quantize_mx(
+                    out=wsrc[w][1][:, sl].bitcast(FP8X4), scales=wsrc[w][2][:, sl],
+                    in_=live["wg", w, hf][:, g * 2048 : (g + 1) * 2048],
+                )
+
+            for g in range(2):
+                at(pos, LAGS["WQ"][0], lambda g=g: qz(g))
+
+        def unit_x(pos, i, engine):
+            lag = LAGS["X"]
+            c = i // 2
+
+            def pe():
+                live["xb", i] = word_transposes(xraw[c], i % 2, "xb%d" % i)
+
+            def ev():
+                if ("xg", c) not in live:
+                    live["xg", c] = grp.tile([P, 2048], BF16, tag="xg", name="xg%d" % c, align_bytes=64)
+                xgv = live["xg", c][:].bitcast(F32).rearrange("p (j g r u) -> p j g r u", j=2, g=2, u=2)
+                copy_on(
+                    engine, xgv[:, i % 2, :, :, :], live["xb", i][:].rearrange("p (g u r) -> p g r u", g=2, u=2)
+                )
+
+            at(pos, lag[0], pe)
+            at(pos, lag[1], ev)
+
+        def unit_xq(pos, c):
+            def qz():
+                sl = slice(c * 512, (c + 1) * 512)
+                nc.vector.quantize_mx(out=xq[:, sl].bitcast(FP8X4), scales=xs[:, sl], in_=live["xg", c][:])
+
+            at(pos, LAGS["XQ"][0], qz)
+
+        def unit_a(pos, br, i, engine):
+            lag = LAGS["A"]
+
+            def pe(hf):
+                ps = pmm.tile([P, 512], F32, tag="mm", name="ps%d_%d_%d" % (br, i, hf))
+                live["ps", br, i, hf] = ps
+                if br == 3:
+                    zc = (i // 4) * D + 512 + (i % 4) * P
+                    nc.tensor.matmul(
+                        out=ps[:], lhsT=zuT[:, zc : zc + P], rhs=zuT[:, hf * D : hf * D + 512],
+                        start=True, stop=True,
                     )
                 else:
-                    nc.vector.tensor_copy(out=dst, in_=ps[:])
-            return bc
+                    for g in range(2):
+                        ls = slice(i * 256 + g * P, i * 256 + (g + 1) * P)
+                        rs = slice(g * 1024 + hf * 512, g * 1024 + hf * 512 + 512)
+                        nc.tensor.matmul_mx(
+                            out=ps[:], lhsT=xq[:, ls].bitcast(FP8X4), lhsT_scale=xs[:, ls],
+                            rhs=u1q[:, rs].bitcast(FP8X4), rhs_scale=u1s[:, rs],
+                            start=(g == 0), stop=(g == 1),
+                        )
 
-        def norm_unit(nm_, ps_pair, bc):
-            v = vnp.tile([P, D], F32, name=nm_)
-            ssum = stat.tile([P, 2], F32, tag="ssum", name="ssum")
-            for hf in range(2):
+            def add_bias(hf):
+                if ("n", br, i) not in live:
+                    live["n", br, i] = vnp.tile([P, D], F32, name="n%d_%d" % (br, i))
+                    live["ssum", br, i] = stat.tile([P, 2], F32, tag="ssum", name="ssum%d_%d" % (br, i))
                 sl = slice(hf * 512, (hf + 1) * 512)
                 nc.vector.scalar_tensor_tensor(
-                    out=v[:, sl], in0=ps_pair[hf][:], scalar=1.0, in1=bc[:, sl],
-                    op0=ALU.mult, op1=ALU.add, accum_out=ssum[:, hf : hf + 1],
+                    out=live["n", br, i][:, sl], in0=live["ps", br, i, hf][:], scalar=1.0, in1=bcs[br][:, sl],
+                    op0=ALU.mult, op1=ALU.add, accum_out=live["ssum", br, i][:, hf : hf + 1],
                 )
-            negmean = stat.tile([P, 1], F32, tag="negmean", name="negmean")
-            nc.gpsimd.tensor_scalar(
-                out=negmean[:], in0=ssum[:, 0:1], scalar1=ssum[:, 1:2], scalar2=-1.0 / D,
-                op0=ALU.add, op1=ALU.mult,
-            )
-            junk = junkp.tile([P, D], BF16, tag="junk", name="junk")
-            sq = stat.tile([P, 1], F32, tag="sq", name="sq")
-            nc.scalar.activation(
-                out=junk[:], in_=v[:], func=ACT.Square, bias=negmean[:, 0:1], scale=1.0, accum_out=sq[:, 0:1]
-            )
-            vare = stat.tile([P, 1], F32, tag="vare", name="vare")
-            nc.gpsimd.tensor_scalar(
-                out=vare[:], in0=sq[:], scalar1=1.0 / D, scalar2=EPS, op0=ALU.mult, op1=ALU.add
-            )
-            rstd = stat.tile([P, 1], F32, tag="rstd", name="rstd")
-            nc.gpsimd.tensor_tensor(out=rstd[:], in0=vare[:], in1=mhalf[:], op=ALU.pow)
-            nc.gpsimd.tensor_scalar(
-                out=v[:], in0=v[:], scalar1=negmean[:, 0:1], scalar2=rstd[:, 0:1], op0=ALU.add, op1=ALU.mult
-            )
-            return v
 
-        def branch3(i):
-            pair = []
-            for hf in range(2):
-                ps = pmm.tile([P, 512], F32, tag="mm", name="ps3")
-                nc.tensor.matmul(
-                    out=ps[:], lhsT=z2T[:, i * P : (i + 1) * P], rhs=u3T[:, hf * 512 : (hf + 1) * 512],
-                    start=True, stop=True,
+            def mean():
+                negmean = stat.tile([P, 1], F32, tag="negmean", name="negmean%d_%d" % (br, i))
+                live["nm", br, i] = negmean
+                ssum = live["ssum", br, i]
+                nc.gpsimd.tensor_scalar(
+                    out=negmean[:], in0=ssum[:, 0:1], scalar1=ssum[:, 1:2], scalar2=-1.0 / D,
+                    op0=ALU.add, op1=ALU.mult,
                 )
-                pair.append(ps)
-            return norm_unit("n3_%d" % i, pair, bc3)
 
-        def branch1(i):
-            pair = []
+            def squares():
+                junk = junkp.tile([P, D], BF16, tag="junk", name="junk%d_%d" % (br, i))
+                sq = stat.tile([P, 1], F32, tag="sq", name="sq%d_%d" % (br, i))
+                live["sq", br, i] = sq
+                nc.scalar.activation(
+                    out=junk[:], in_=live["n", br, i][:], func=ACT.Square, bias=live["nm", br, i][:, 0:1],
+                    scale=1.0, accum_out=sq[:, 0:1],
+                )
+
+            def rstd_():
+                vare = stat.tile([P, 1], F32, tag="vare", name="vare%d_%d" % (br, i))
+                nc.gpsimd.tensor_scalar(
+                    out=vare[:], in0=live["sq", br, i][:], scalar1=1.0 / D, scalar2=EPS, op0=ALU.mult, op1=ALU.add
+                )
+                rstd = stat.tile([P, 1], F32, tag="rstd", name="rstd%d_%d" % (br, i))
+                live["rstd", br, i] = rstd
+                nc.gpsimd.tensor_tensor(out=rstd[:], in0=vare[:], in1=mhalf[:], op=ALU.pow)
+
+            def normalise():
+                v = live["n", br, i]
+                eng = nc.gpsimd if engine == "pool" else nc.vector
+                eng.tensor_scalar(
+                    out=v[:], in0=v[:], scalar1=live["nm", br, i][:, 0:1], scalar2=live["rstd", br, i][:, 0:1],
+                    op0=ALU.add, op1=ALU.mult,
+                )
+
             for hf in range(2):
-                ps = pmm.tile([P, 512], F32, tag="mm", name="ps1")
-                for g in range(2):
-                    ls = slice(i * 256 + g * P, i * 256 + (g + 1) * P)
-                    rs = slice(g * 1024 + hf * 512, g * 1024 + hf * 512 + 512)
-                    nc.tensor.matmul_mx(
-                        out=ps[:], lhsT=xq[:, ls].bitcast(FP8X4), lhsT_scale=xs[:, ls],
-                        rhs=u1q[:, rs].bitcast(FP8X4), rhs_scale=u1s[:, rs],
-                        start=(g == 0), stop=(g == 1),
+                at(pos, lag[0], lambda hf=hf: pe(hf))
+                at(pos, lag[1], lambda hf=hf: add_bias(hf))
+            for (k, fn) in enumerate((mean, squares, rstd_, normalise)):
+                at(pos, lag[2 + k], fn)
+
+        def unit_cols(pos):
+            lag = LAGS["COLS"]
+
+            def pe():
+                pv = ptp.tile([P, 512], F32, tag="tp", name="pv")
+                live["pv"] = pv
+                nc.tensor.transpose(out=pv[:, 0:P], in_=vrows[:], identity=identF[:])
+
+            def ev():
+                vw = const.tile([P, 16], F32, name="vw")
+                nc.vector.tensor_copy(out=vw[:], in_=live["pv"][:, 0:16])
+                nc.vector.tensor_copy(out=cols[:], in_=vw[:].bitcast(BF16))
+                al = const.tile([P, 1], F32, name="al")
+                nc.vector.tensor_copy(out=al[:], in_=al_bf[:])
+                nc.vector.tensor_scalar(
+                    out=g3p[:], in0=cols[:, 16:24], scalar1=al[:, 0:1], scalar2=None, op0=ALU.mult
+                )
+                nc.vector.tensor_scalar(
+                    out=b3p[:], in0=cols[:, 24:32], scalar1=al[:, 0:1], scalar2=1.0, op0=ALU.mult, op1=ALU.add
+                )
+
+            at(pos, lag[0], pe)
+            at(pos, lag[1], ev)
+
+        def unit_b(pos, i0, ntl, g, t, engine):
+            lag = LAGS["B"]
+            jt = 4 * g + t
+            tg = ntl * P
+
+            def pe(br):
+                bank = ptp.tile([P, 512], F32, tag="tp", name="nb%d_%d_%d" % (br, i0, jt))
+                live["nb", br, i0, jt] = bank
+                for il in range(ntl):
+                    nc.tensor.transpose(
+                        out=bank[:, il * P : (il + 1) * P],
+                        in_=live["n", br, i0 + il][:, jt * P : (jt + 1) * P],
+                        identity=identF[:],
                     )
-                pair.append(ps)
-            return norm_unit("n1_%d" % i, pair, bc1)
 
-        def gate_group(grp_i):
-            for g in range(2):
-                o1 = op.tile([P, 4, 512], F32, tag="o1", name="o1")
-                o3 = op.tile([P, 4, 512], F32, tag="o3", name="o3")
-                for t in range(4):
-                    jt = 4 * g + t
-                    for (ns, dst, gcol, bcol) in (
-                        (n1, o1, cols[:, jt : jt + 1], cols[:, 8 + jt : 9 + jt]),
-                        (n3, o3, g3p[:, jt : jt + 1], b3p[:, jt : jt + 1]),
-                    ):
-                        bank = ptp.tile([P, 512], F32, tag="tp", name="nbank")
-                        for il in range(4):
-                            nc.tensor.transpose(
-                                out=bank[:, il * P : (il + 1) * P],
-                                in_=ns[4 * grp_i + il][:, jt * P : (jt + 1) * P],
-                                identity=identF[:],
-                            )
-                        nc.scalar.activation(
-                            out=dst[:, t, :], in_=bank[:], func=ACT.Identity, bias=bcol, scale=gcol
-                        )
-                hg = grp.tile([P, 2048], BF16, tag="hg", name="hg", align_bytes=64)
+            def affine(br):
+                if ("o", br, i0, g) not in live:
+                    live["o", br, i0, g] = op.tile([P, 4, tg], F32, tag="o%d" % br, name="o%d_%d_%d" % (br, i0, g))
+                gcol = cols[:, jt : jt + 1] if br == 1 else g3p[:, jt : jt + 1]
+                bcol = cols[:, 8 + jt : 9 + jt] if br == 1 else b3p[:, jt : jt + 1]
+                dst = live["o", br, i0, g][:, t, :]
+                src = live["nb", br, i0, jt][:, 0:tg]
+                if engine == "act":
+                    nc.scalar.activation(out=dst, in_=src, func=ACT.Identity, bias=bcol, scale=gcol)
+                else:
+                    nc.vector.tensor_scalar(out=dst, in0=src, scalar1=gcol, scalar2=bcol, op0=ALU.mult, op1=ALU.add)
+
+            for br in (3, 1):
+                at(pos, lag[0], lambda br=br: pe(br))
+                at(pos, lag[1], lambda br=br: affine(br))
+
+        def unit_f(pos, i0, ntl, g):
+            lag = LAGS["F"]
+            tg = ntl * P
+
+            def gate():
+                hg = grp.tile([P, 4 * tg], BF16, tag="hg", name="hg%d_%d" % (i0, g), align_bytes=64)
+                live["hg", i0, g] = hg
                 nc.vector.tensor_tensor(
                     out=hg[:].rearrange("p (c i t) -> p c t i", i=4, t=4),
-                    in0=o1[:].rearrange("p t (c i) -> p c t i", i=4),
-                    in1=o3[:].rearrange("p t (c i) -> p c t i", i=4),
+                    in0=live["o", 1, i0, g][:].rearrange("p t (c i) -> p c t i", i=4),
+                    in1=live["o", 3, i0, g][:].rearrange("p t (c i) -> p c t i", i=4),
                     op=ALU.mult,
                 )
-                sl = slice(g * 1024 + grp_i * 512, g * 1024 + grp_i * 512 + 512)
-                nc.vector.quantize_mx(out=hq[:, sl].bitcast(FP8X4), scales=hs[:, sl], in_=hg[:])
 
-        def stage2(i):
-            ot = otp.tile([P, D], F32, tag="ot", name="ot")
-            for hf in range(2):
-                ps = pmm.tile([P, 512], F32, tag="mm", name="ps2")
+            def qz():
+                sl = slice(g * 1024 + i0 * P, g * 1024 + i0 * P + tg)
+                nc.vector.quantize_mx(out=hq[:, sl].bitcast(FP8X4), scales=hs[:, sl], in_=live["hg", i0, g][:])
+
+            at(pos, lag[0], gate)
+            at(pos, lag[1], qz)
+
+        def unit_s(pos, i):
+            lag = LAGS["S"]
+
+            def pe(hf):
+                ps = pmm.tile([P, 512], F32, tag="mm", name="ps2_%d_%d" % (i, hf))
+                live["ps2", i, hf] = ps
                 for g in range(2):
                     ls = slice(g * 1024 + i * P, g * 1024 + (i + 1) * P)
                     rs = slice(g * 1024 + hf * 512, g * 1024 + hf * 512 + 512)
@@ -246,69 +426,28 @@ def tile_polymlp_skiplora_pa_kernel(
                         rhs=cq[:, rs].bitcast(FP8X4), rhs_scale=cs[:, rs],
                         start=(g == 0), stop=(g == 1),
                     )
-                sl = slice(hf * 512, (hf + 1) * 512)
-                nc.vector.tensor_tensor(out=ot[:, sl], in0=ps[:], in1=bcc[:, sl], op=ALU.add)
-            nc.sync.dma_start(out=o_v[:, i, :], in_=ot[:])
 
-        z2T = const.tile([P, D], BF16)
-        u3T = const.tile([P, D], BF16)
-        for (raw, dstT) in ((z2raw, z2T), (u3raw, u3T)):
-            pb = ptp.tile([P, D], BF16, tag="tp", name="pb")
-            for k in range(8):
-                nc.tensor.transpose(
-                    out=pb[:, k * P : (k + 1) * P], in_=raw[:, k * P : (k + 1) * P], identity=identB[:]
+            def add_bias(hf):
+                if ("ot", i) not in live:
+                    live["ot", i] = otp.tile([P, D], F32, tag="ot", name="ot%d" % i)
+                sl = slice(hf * 512, (hf + 1) * 512)
+                nc.vector.tensor_tensor(
+                    out=live["ot", i][:, sl], in0=live["ps2", i, hf][:], in1=bcc[:, sl], op=ALU.add
                 )
-            nc.scalar.copy(out=dstT[:], in_=pb[:])
-        bc3 = bias_plane(brow3, "bc3", True)
-        n1 = []
-        n3 = []
-        for i in range(4):
-            n3.append(branch3(i))
-        prep_weight(u1raw, u1q, u1s, ("act", "dve"))
-        bc1 = bias_plane(brow1, "bc1", True)
-        xraw.append(load_raw(x_v[2], "xraw2", False))
-        xraw.append(load_raw(x_v[3], "xraw3", False))
-        for v, vec in enumerate((ln1_g, ln1_b, ln3_g, ln3_b)):
-            nc.sync.dma_start(
-                out=vrows[4 * v : 4 * v + 4, :].bitcast(BF16), in_=vec.rearrange("(r w) -> r w", r=4)
-            )
-        al_bf = const.tile([P, 1], BF16)
-        nc.sync.dma_start(out=al_bf[:], in_=alpha.partition_broadcast(P))
-        browc = bias_row(C_b)
-        craw = [load_raw(c_v[c], "craw%d" % c, True) for c in range(2)]
-        prep_x(0)
-        prep_x(1)
-        craw.append(load_raw(c_v[2], "craw2", True))
-        craw.append(load_raw(c_v[3], "craw3", True))
-        for i in range(4):
-            n1.append(branch1(i))
-        pv = ptp.tile([P, 512], F32, tag="tp", name="pv")
-        nc.tensor.transpose(out=pv[:, 0:P], in_=vrows[:], identity=identF[:])
-        vw = const.tile([P, 16], F32)
-        nc.vector.tensor_copy(out=vw[:], in_=pv[:, 0:16])
-        cols = const.tile([P, 32], F32)
-        nc.vector.tensor_copy(out=cols[:], in_=vw[:].bitcast(BF16))
-        al = const.tile([P, 1], F32)
-        nc.vector.tensor_copy(out=al[:], in_=al_bf[:])
-        g3p = const.tile([P, 8], F32)
-        nc.vector.tensor_scalar(
-            out=g3p[:], in0=cols[:, 16:24], scalar1=al[:, 0:1], scalar2=None, op0=ALU.mult
-        )
-        b3p = const.tile([P, 8], F32)
-        nc.vector.tensor_scalar(
-            out=b3p[:], in0=cols[:, 24:32], scalar1=al[:, 0:1], scalar2=1.0, op0=ALU.mult, op1=ALU.add
-        )
-        prep_x(2)
-        prep_x(3)
-        for i in range(4, 8):
-            n3.append(branch3(i))
-        prep_weight(craw, cq, cs, ("act",))
-        bcc = bias_plane(browc, "bcc", False)
-        for i in range(4, 8):
-            n1.append(branch1(i))
-        gate_group(0)
-        for i in range(4):
-            stage2(i)
-        gate_group(1)
-        for i in range(4, 8):
-            stage2(i)
+
+            def store():
+                nc.sync.dma_start(out=o_v[:, i, :], in_=live["ot", i][:])
+
+            for hf in range(2):
+                at(pos, lag[0], lambda hf=hf: pe(hf))
+                at(pos, lag[1], lambda hf=hf: add_bias(hf))
+            at(pos, lag[2], store)
+
+        builders = {
+            "ZU": unit_zu, "BC": unit_bc, "W": unit_w, "WQ": unit_wq, "X": unit_x, "XQ": unit_xq,
+            "A": unit_a, "COLS": unit_cols, "B": unit_b, "F": unit_f, "S": unit_s,
+        }
+        for pos, unit in enumerate(PROGRAM):
+            builders[unit[0]](pos, *unit[1:])
+        for seq in ORDER:
+            ops[seq][2]()

@@ -18,19 +18,19 @@ EPS = 1e-6
 FLOPS = 2 * 1024 * (1024 * 1024 * 2 + 128 * 1024)
 PINNED = True
 PROGRAM = (
-    ('ZU', 0), ('BC', 3), ('ZU', 1), ('A', 3, 0, 'pool'), ('A', 3, 1, 'pool'), ('W', 'U', 0, 'act'),
-    ('W', 'U', 1, 'dve'), ('A', 3, 2, 'pool'), ('W', 'U', 2, 'act'), ('W', 'U', 3, 'dve'), ('WQ', 'U', 0), ('A', 3, 3, 'pool'),
+    ('ZU', 0), ('BC', 3), ('ZU', 1), ('A', 3, 0, 'dve'), ('A', 3, 1, 'dve'), ('W', 'U', 0, 'act'),
+    ('W', 'U', 1, 'dve'), ('A', 3, 2, 'dve'), ('W', 'U', 2, 'act'), ('W', 'U', 3, 'dve'), ('WQ', 'U', 0), ('A', 3, 3, 'dve'),
     ('W', 'U', 4, 'act'), ('W', 'U', 5, 'dve'), ('W', 'U', 6, 'act'), ('W', 'U', 7, 'dve'), ('WQ', 'U', 1), ('BC', 1),
-    ('X', 0, 'act'), ('X', 1, 'act'), ('XQ', 0), ('A', 1, 0, 'pool'), ('A', 1, 1, 'pool'), ('X', 2, 'act'),
-    ('X', 3, 'act'), ('XQ', 1), ('COLS',), ('A', 1, 2, 'pool'), ('A', 1, 3, 'pool'), ('X', 4, 'act'),
+    ('X', 0, 'act'), ('X', 1, 'act'), ('XQ', 0), ('A', 1, 0, 'dve'), ('A', 1, 1, 'dve'), ('X', 2, 'act'),
+    ('X', 3, 'act'), ('XQ', 1), ('COLS',), ('A', 1, 2, 'dve'), ('A', 1, 3, 'dve'), ('X', 4, 'act'),
     ('X', 5, 'act'), ('XQ', 2), ('X', 6, 'act'), ('X', 7, 'act'), ('XQ', 3), ('B', 0, 2, 0, 0, 'act'),
     ('B', 0, 2, 0, 1, 'act'), ('B', 0, 2, 0, 2, 'act'), ('B', 0, 2, 0, 3, 'act'), ('F', 0, 2, 0), ('B', 0, 2, 1, 0, 'act'), ('B', 0, 2, 1, 1, 'act'),
-    ('B', 0, 2, 1, 2, 'act'), ('B', 0, 2, 1, 3, 'act'), ('F', 0, 2, 1), ('A', 3, 4, 'pool'), ('A', 3, 5, 'pool'), ('W', 'C', 0, 'act'),
+    ('B', 0, 2, 1, 2, 'act'), ('B', 0, 2, 1, 3, 'act'), ('F', 0, 2, 1), ('A', 3, 4, 'dve'), ('A', 3, 5, 'dve'), ('W', 'C', 0, 'act'),
     ('W', 'C', 1, 'act'), ('W', 'C', 2, 'act'), ('W', 'C', 3, 'act'), ('WQ', 'C', 0), ('W', 'C', 4, 'act'), ('W', 'C', 5, 'act'),
-    ('W', 'C', 6, 'act'), ('W', 'C', 7, 'act'), ('WQ', 'C', 1), ('A', 1, 4, 'pool'), ('A', 1, 5, 'pool'), ('B', 2, 2, 0, 0, 'act'),
+    ('W', 'C', 6, 'act'), ('W', 'C', 7, 'act'), ('WQ', 'C', 1), ('A', 1, 4, 'dve'), ('A', 1, 5, 'dve'), ('B', 2, 2, 0, 0, 'act'),
     ('B', 2, 2, 0, 1, 'act'), ('B', 2, 2, 0, 2, 'act'), ('B', 2, 2, 0, 3, 'act'), ('F', 2, 2, 0), ('B', 2, 2, 1, 0, 'act'), ('B', 2, 2, 1, 1, 'act'),
-    ('B', 2, 2, 1, 2, 'act'), ('B', 2, 2, 1, 3, 'act'), ('F', 2, 2, 1), ('S', 0), ('S', 1), ('A', 3, 6, 'pool'),
-    ('A', 3, 7, 'pool'), ('A', 1, 6, 'pool'), ('A', 1, 7, 'pool'), ('S', 2), ('S', 3), ('B', 4, 2, 0, 0, 'act'),
+    ('B', 2, 2, 1, 2, 'act'), ('B', 2, 2, 1, 3, 'act'), ('F', 2, 2, 1), ('S', 0), ('S', 1), ('A', 3, 6, 'dve'),
+    ('A', 3, 7, 'dve'), ('A', 1, 6, 'dve'), ('A', 1, 7, 'dve'), ('S', 2), ('S', 3), ('B', 4, 2, 0, 0, 'act'),
     ('B', 4, 2, 0, 1, 'act'), ('B', 4, 2, 0, 2, 'act'), ('B', 4, 2, 0, 3, 'act'), ('F', 4, 2, 0), ('B', 4, 2, 1, 0, 'act'), ('B', 4, 2, 1, 1, 'act'),
     ('B', 4, 2, 1, 2, 'act'), ('B', 4, 2, 1, 3, 'act'), ('F', 4, 2, 1), ('S', 4), ('S', 5), ('B', 6, 2, 0, 0, 'act'),
     ('B', 6, 2, 0, 1, 'act'), ('B', 6, 2, 0, 2, 'act'), ('B', 6, 2, 0, 3, 'act'), ('F', 6, 2, 0), ('B', 6, 2, 1, 0, 'act'), ('B', 6, 2, 1, 1, 'act'),
@@ -38,22 +38,22 @@ PROGRAM = (
 )
 LAGS = {'ZU': (0, 0, 0, 0, 0, 0, 0, 0), 'BC': (0, 0, 0, 0, 0, 0, 0, 0), 'W': (0, 0, 0, 0, 0, 0, 0, 0), 'WQ': (0, 0, 0, 0, 0, 0, 0, 0), 'X': (0, 0, 0, 0, 0, 0, 0, 0), 'XQ': (0, 0, 0, 0, 0, 0, 0, 0), 'A': (0, 0, 0, 0, 0, 0, 0, 0), 'COLS': (0, 0, 0, 0, 0, 0, 0, 0), 'B': (0, 0, 0, 0, 0, 0, 0, 0), 'F': (0, 0, 0, 0, 0, 0, 0, 0), 'S': (0, 0, 0, 0, 0, 0, 0, 0)}
 ORDER = (
-    0, 2, 4, 1, 6, 3, 5, 8, 16, 7, 24, 9, 10, 17, 18, 26, 11, 25, 28, 19, 30, 12, 13, 36,
-    27, 20, 38, 29, 42, 21, 14, 44, 31, 50, 15, 39, 52, 37, 43, 54, 51, 40, 56, 22, 55, 41, 60, 23,
-    62, 45, 64, 53, 66, 65, 57, 85, 32, 67, 46, 58, 87, 33, 59, 90, 108, 61, 154, 47, 63, 156, 34, 162,
-    68, 35, 164, 91, 86, 110, 155, 88, 113, 157, 109, 69, 48, 89, 111, 71, 49, 70, 115, 72, 114, 77, 112, 79,
-    73, 158, 74, 78, 118, 122, 80, 92, 116, 75, 163, 94, 119, 76, 93, 123, 100, 159, 95, 126, 102, 101, 130, 81,
-    96, 82, 160, 136, 103, 140, 161, 190, 117, 192, 97, 165, 198, 191, 83, 200, 127, 193, 131, 84, 144, 137, 199, 148,
-    141, 170, 145, 201, 149, 172, 171, 98, 174, 120, 173, 124, 99, 121, 128, 125, 132, 138, 129, 133, 142, 139, 134, 104,
-    146, 166, 175, 194, 150, 202, 252, 105, 176, 135, 253, 254, 260, 143, 262, 255, 106, 268, 147, 180, 151, 107, 261, 167,
-    182, 152, 184, 177, 168, 153, 270, 181, 263, 186, 169, 183, 178, 206, 185, 179, 208, 187, 276, 269, 210, 256, 264, 195,
-    242, 188, 212, 189, 247, 203, 196, 243, 197, 248, 244, 207, 271, 249, 209, 214, 211, 245, 216, 213, 218, 215, 204, 277,
-    246, 220, 217, 224, 219, 205, 226, 221, 228, 225, 222, 230, 227, 232, 229, 234, 231, 236, 272, 223, 233, 238, 235, 237,
-    278, 239, 250, 257, 294, 240, 296, 251, 298, 300, 265, 258, 241, 279, 284, 259, 286, 273, 285, 289, 287, 291, 266, 295,
-    290, 297, 288, 302, 267, 299, 304, 292, 301, 306, 303, 308, 293, 305, 312, 307, 314, 309, 316, 274, 313, 310, 318, 315,
-    320, 275, 317, 322, 319, 324, 311, 321, 326, 323, 340, 325, 344, 327, 348, 280, 341, 328, 352, 281, 358, 329, 345, 330,
-    282, 349, 353, 332, 283, 359, 331, 335, 333, 337, 336, 334, 362, 342, 338, 346, 363, 350, 343, 339, 354, 347, 360, 351,
-    364, 355, 366, 361, 356, 368, 365, 370, 367, 372, 369, 357, 371, 373, 374, 375, 376, 378, 377, 381, 379, 383, 382, 380,
+    0, 2, 1, 4, 3, 6, 5, 8, 16, 7, 24, 9, 26, 10, 25, 17, 18, 28, 11, 30, 36, 12, 19, 13,
+    38, 42, 20, 27, 50, 44, 29, 52, 21, 14, 15, 60, 31, 37, 22, 51, 23, 62, 54, 32, 56, 39, 33, 40,
+    64, 41, 55, 34, 35, 65, 66, 43, 85, 67, 45, 154, 86, 46, 53, 87, 47, 57, 90, 108, 58, 110, 59, 88,
+    156, 48, 49, 111, 113, 61, 63, 115, 68, 162, 116, 89, 69, 109, 91, 155, 114, 118, 70, 71, 119, 112, 77, 117,
+    122, 72, 126, 130, 123, 136, 73, 78, 127, 79, 74, 157, 140, 92, 80, 94, 131, 137, 75, 76, 100, 81, 93, 82,
+    144, 148, 170, 95, 102, 96, 101, 141, 164, 97, 172, 83, 84, 190, 103, 145, 149, 98, 120, 99, 171, 192, 104, 158,
+    124, 163, 105, 128, 165, 198, 166, 191, 121, 200, 125, 132, 129, 106, 107, 138, 159, 142, 252, 193, 194, 199, 254, 133,
+    139, 146, 134, 260, 143, 150, 147, 174, 167, 176, 135, 160, 161, 151, 201, 173, 180, 152, 262, 175, 182, 177, 184, 153,
+    181, 168, 169, 186, 183, 178, 206, 185, 179, 208, 187, 210, 202, 253, 195, 212, 188, 242, 189, 203, 196, 197, 243, 207,
+    204, 205, 244, 209, 211, 255, 214, 213, 216, 218, 215, 220, 256, 261, 217, 224, 219, 263, 226, 221, 228, 247, 225, 222,
+    227, 230, 229, 232, 234, 257, 223, 236, 245, 249, 231, 248, 246, 268, 233, 238, 250, 235, 237, 270, 264, 239, 251, 269,
+    265, 276, 240, 278, 294, 296, 241, 298, 295, 300, 258, 259, 284, 297, 299, 266, 267, 302, 301, 304, 306, 271, 303, 308,
+    305, 312, 272, 277, 286, 307, 273, 279, 314, 289, 280, 285, 291, 281, 274, 275, 316, 287, 309, 282, 313, 283, 288, 318,
+    315, 320, 290, 317, 322, 319, 324, 292, 321, 326, 323, 340, 310, 293, 325, 342, 327, 344, 346, 345, 311, 341, 348, 328,
+    343, 350, 347, 352, 349, 354, 351, 329, 358, 353, 330, 355, 359, 356, 332, 357, 331, 335, 333, 337, 336, 334, 360, 362,
+    338, 364, 361, 366, 363, 339, 368, 365, 370, 367, 372, 369, 371, 373, 374, 375, 376, 378, 377, 381, 379, 383, 382, 380,
     384, 385,
 )
 
@@ -114,8 +114,10 @@ def tile_polymlp_skiplora_pa_kernel(
             return t
 
         brows = {3: bias_row(U3_b, "brow3")}
-        mhalf = const.tile([P, 1], F32)
-        nc.vector.memset(mhalf[:], -0.5)
+        epsc = const.tile([P, 1], F32)
+        nc.vector.memset(epsc[:], EPS)
+        warm = const.tile([P, 1], F32)
+        nc.scalar.activation(out=warm[:], in_=epsc[:], func=ACT.Sqrt)
         vrows = const.tile([P, P], F32)
         nc.vector.memset(vrows[:], 0.0)
         u1raw = [load_raw(u1_v[a], "u1raw%d" % a, False) for a in range(4)]
@@ -299,7 +301,7 @@ def tile_polymlp_skiplora_pa_kernel(
                 negmean = stat.tile([P, 1], F32, tag="negmean", name="negmean%d_%d" % (br, i))
                 live["nm", br, i] = negmean
                 ssum = live["ssum", br, i]
-                nc.gpsimd.tensor_scalar(
+                nc.vector.tensor_scalar(
                     out=negmean[:], in0=ssum[:, 0:1], scalar1=ssum[:, 1:2], scalar2=-1.0 / D,
                     op0=ALU.add, op1=ALU.mult,
                 )
@@ -307,28 +309,36 @@ def tile_polymlp_skiplora_pa_kernel(
             def squares():
                 junk = junkp.tile([P, D], BF16, tag="junk", name="junk%d_%d" % (br, i))
                 sq = stat.tile([P, 1], F32, tag="sq", name="sq%d_%d" % (br, i))
-                live["sq", br, i] = sq
                 nc.scalar.activation(
                     out=junk[:], in_=live["n", br, i][:], func=ACT.Square, bias=live["nm", br, i][:, 0:1],
                     scale=1.0, accum_out=sq[:, 0:1],
                 )
+                std = stat.tile([P, 1], F32, tag="std", name="std%d_%d" % (br, i))
+                live["std", br, i] = std
+                nc.scalar.activation(out=std[:], in_=sq[:], func=ACT.Sqrt, bias=epsc[:, 0:1], scale=1.0 / D)
 
             def rstd_():
-                vare = stat.tile([P, 1], F32, tag="vare", name="vare%d_%d" % (br, i))
-                nc.gpsimd.tensor_scalar(
-                    out=vare[:], in0=live["sq", br, i][:], scalar1=1.0 / D, scalar2=EPS, op0=ALU.mult, op1=ALU.add
-                )
                 rstd = stat.tile([P, 1], F32, tag="rstd", name="rstd%d_%d" % (br, i))
                 live["rstd", br, i] = rstd
-                nc.gpsimd.tensor_tensor(out=rstd[:], in0=vare[:], in1=mhalf[:], op=ALU.pow)
+                nc.vector.reciprocal(out=rstd[:], in_=live["std", br, i][:])
+                if engine == "act":
+                    nmr = stat.tile([P, 1], F32, tag="nmr", name="nmr%d_%d" % (br, i))
+                    live["nmr", br, i] = nmr
+                    nc.vector.tensor_tensor(out=nmr[:], in0=live["nm", br, i][:], in1=rstd[:], op=ALU.mult)
 
             def normalise():
                 v = live["n", br, i]
-                eng = nc.gpsimd if engine == "pool" else nc.vector
-                eng.tensor_scalar(
-                    out=v[:], in0=v[:], scalar1=live["nm", br, i][:, 0:1], scalar2=live["rstd", br, i][:, 0:1],
-                    op0=ALU.add, op1=ALU.mult,
-                )
+                if engine == "act":
+                    nc.scalar.activation(
+                        out=v[:], in_=v[:], func=ACT.Identity, bias=live["nmr", br, i][:, 0:1],
+                        scale=live["rstd", br, i][:, 0:1],
+                    )
+                else:
+                    eng = nc.gpsimd if engine == "pool" else nc.vector
+                    eng.tensor_scalar(
+                        out=v[:], in0=v[:], scalar1=live["nm", br, i][:, 0:1], scalar2=live["rstd", br, i][:, 0:1],
+                        op0=ALU.add, op1=ALU.mult,
+                    )
 
             for hf in range(2):
                 at(pos, lag[0], lambda hf=hf: pe(hf))

@@ -17,45 +17,108 @@ D = 1024
 EPS = 1e-6
 FLOPS = 2 * 1024 * (1024 * 1024 * 2 + 128 * 1024)
 PINNED = True
-PROGRAM = (
-    ('ZU', 0), ('BC', 3), ('ZU', 1), ('A', 3, 0, 'dve'), ('A', 3, 1, 'dve'), ('W', 'U', 0, 'act'),
-    ('W', 'U', 1, 'dve'), ('A', 3, 2, 'dve'), ('W', 'U', 2, 'act'), ('W', 'U', 3, 'dve'), ('WQ', 'U', 0), ('A', 3, 3, 'dve'),
-    ('W', 'U', 4, 'act'), ('W', 'U', 5, 'dve'), ('W', 'U', 6, 'act'), ('W', 'U', 7, 'dve'), ('WQ', 'U', 1), ('BC', 1),
-    ('X', 0, 'act'), ('X', 1, 'act'), ('XQ', 0), ('A', 1, 0, 'dve'), ('A', 1, 1, 'dve'), ('X', 2, 'act'),
-    ('X', 3, 'act'), ('XQ', 1), ('COLS',), ('A', 1, 2, 'dve'), ('A', 1, 3, 'dve'), ('X', 4, 'act'),
-    ('X', 5, 'act'), ('XQ', 2), ('X', 6, 'act'), ('X', 7, 'act'), ('XQ', 3), ('B', 0, 2, 0, 0, 'act'),
-    ('B', 0, 2, 0, 1, 'act'), ('B', 0, 2, 0, 2, 'act'), ('B', 0, 2, 0, 3, 'act'), ('F', 0, 2, 0), ('B', 0, 2, 1, 0, 'act'), ('B', 0, 2, 1, 1, 'act'),
-    ('B', 0, 2, 1, 2, 'act'), ('B', 0, 2, 1, 3, 'act'), ('F', 0, 2, 1), ('A', 3, 4, 'dve'), ('A', 3, 5, 'dve'), ('W', 'C', 0, 'act'),
-    ('W', 'C', 1, 'act'), ('W', 'C', 2, 'act'), ('W', 'C', 3, 'act'), ('WQ', 'C', 0), ('W', 'C', 4, 'act'), ('W', 'C', 5, 'act'),
-    ('W', 'C', 6, 'act'), ('W', 'C', 7, 'act'), ('WQ', 'C', 1), ('A', 1, 4, 'dve'), ('A', 1, 5, 'dve'), ('B', 2, 2, 0, 0, 'act'),
-    ('B', 2, 2, 0, 1, 'act'), ('B', 2, 2, 0, 2, 'act'), ('B', 2, 2, 0, 3, 'act'), ('F', 2, 2, 0), ('B', 2, 2, 1, 0, 'act'), ('B', 2, 2, 1, 1, 'act'),
-    ('B', 2, 2, 1, 2, 'act'), ('B', 2, 2, 1, 3, 'act'), ('F', 2, 2, 1), ('S', 0), ('S', 1), ('A', 3, 6, 'dve'),
-    ('A', 3, 7, 'dve'), ('A', 1, 6, 'dve'), ('A', 1, 7, 'dve'), ('S', 2), ('S', 3), ('B', 4, 2, 0, 0, 'act'),
-    ('B', 4, 2, 0, 1, 'act'), ('B', 4, 2, 0, 2, 'act'), ('B', 4, 2, 0, 3, 'act'), ('F', 4, 2, 0), ('B', 4, 2, 1, 0, 'act'), ('B', 4, 2, 1, 1, 'act'),
-    ('B', 4, 2, 1, 2, 'act'), ('B', 4, 2, 1, 3, 'act'), ('F', 4, 2, 1), ('S', 4), ('S', 5), ('B', 6, 2, 0, 0, 'act'),
-    ('B', 6, 2, 0, 1, 'act'), ('B', 6, 2, 0, 2, 'act'), ('B', 6, 2, 0, 3, 'act'), ('F', 6, 2, 0), ('B', 6, 2, 1, 0, 'act'), ('B', 6, 2, 1, 1, 'act'),
-    ('B', 6, 2, 1, 2, 'act'), ('B', 6, 2, 1, 3, 'act'), ('F', 6, 2, 1), ('S', 6), ('S', 7),
-)
-LAGS = {'ZU': (0, 0, 0, 0, 0, 0, 0, 0), 'BC': (0, 0, 0, 0, 0, 0, 0, 0), 'W': (0, 0, 0, 0, 0, 0, 0, 0), 'WQ': (0, 0, 0, 0, 0, 0, 0, 0), 'X': (0, 0, 0, 0, 0, 0, 0, 0), 'XQ': (0, 0, 0, 0, 0, 0, 0, 0), 'A': (0, 0, 0, 0, 0, 0, 0, 0), 'COLS': (0, 0, 0, 0, 0, 0, 0, 0), 'B': (0, 0, 0, 0, 0, 0, 0, 0), 'F': (0, 0, 0, 0, 0, 0, 0, 0), 'S': (0, 0, 0, 0, 0, 0, 0, 0)}
-ORDER = (
-    0, 2, 1, 4, 3, 6, 5, 8, 16, 7, 24, 9, 26, 10, 25, 17, 18, 28, 11, 30, 36, 12, 19, 13,
-    38, 42, 20, 27, 50, 44, 29, 52, 21, 14, 15, 60, 31, 37, 22, 51, 23, 62, 54, 32, 56, 39, 33, 40,
-    64, 41, 55, 34, 35, 65, 66, 43, 85, 67, 45, 154, 86, 46, 53, 87, 47, 57, 90, 108, 58, 110, 59, 88,
-    156, 48, 49, 111, 113, 61, 63, 115, 68, 162, 116, 89, 69, 109, 91, 155, 114, 118, 70, 71, 119, 112, 77, 117,
-    122, 72, 126, 130, 123, 136, 73, 78, 127, 79, 74, 157, 140, 92, 80, 94, 131, 137, 75, 76, 100, 81, 93, 82,
-    144, 148, 170, 95, 102, 96, 101, 141, 164, 97, 172, 83, 84, 190, 103, 145, 149, 98, 120, 99, 171, 192, 104, 158,
-    124, 163, 105, 128, 165, 198, 166, 191, 121, 200, 125, 132, 129, 106, 107, 138, 159, 142, 252, 193, 194, 199, 254, 133,
-    139, 146, 134, 260, 143, 150, 147, 174, 167, 176, 135, 160, 161, 151, 201, 173, 180, 152, 262, 175, 182, 177, 184, 153,
-    181, 168, 169, 186, 183, 178, 206, 185, 179, 208, 187, 210, 202, 253, 195, 212, 188, 242, 189, 203, 196, 197, 243, 207,
-    204, 205, 244, 209, 211, 255, 214, 213, 216, 218, 215, 220, 256, 261, 217, 224, 219, 263, 226, 221, 228, 247, 225, 222,
-    227, 230, 229, 232, 234, 257, 223, 236, 245, 249, 231, 248, 246, 268, 233, 238, 250, 235, 237, 270, 264, 239, 251, 269,
-    265, 276, 240, 278, 294, 296, 241, 298, 295, 300, 258, 259, 284, 297, 299, 266, 267, 302, 301, 304, 306, 271, 303, 308,
-    305, 312, 272, 277, 286, 307, 273, 279, 314, 289, 280, 285, 291, 281, 274, 275, 316, 287, 309, 282, 313, 283, 288, 318,
-    315, 320, 290, 317, 322, 319, 324, 292, 321, 326, 323, 340, 310, 293, 325, 342, 327, 344, 346, 345, 311, 341, 348, 328,
-    343, 350, 347, 352, 349, 354, 351, 329, 358, 353, 330, 355, 359, 356, 332, 357, 331, 335, 333, 337, 336, 334, 360, 362,
-    338, 364, 361, 366, 363, 339, 368, 365, 370, 367, 372, 369, 371, 373, 374, 375, 376, 378, 377, 381, 379, 383, 382, 380,
-    384, 385,
-)
+NBIG = 20
+GROUPS = ((0, 2), (2, 2), (4, 2), (6, 2))
+NORM_ENGINE = {}
+LT = 1
+LS = 3
+LR = 4
+FAST = 10
+B0 = 15
+SPE = 3
+SADD = 3
+NDVE = (0, 2, 2, 0, 0, 0, 0, 0)
+EVD = (("C", 6),)
+
+
+def plan():
+    head = [("zu.pe", 0), ("bc.pe", 3, 0), ("bc.pe", 3, 1), ("zu.pe", 1), ("zu.ev", 0), ("bc.ev", 3, 0),
+            ("bc.ev", 3, 1), ("zu.ev", 1)]
+    units = [(3, i) for i in range(NT)] + [(1, i) for i in range(NT)]
+    banks = [("w", "U", j) for j in range(8)] + [("x", i) for i in range(NT)] + [("w", "C", j) for j in range(8)]
+    nslot = len(units)
+
+    def upto(s):
+        return min(len(banks), 2 * s if s <= FAST else 2 * FAST + (s - FAST))
+
+    def share(s):
+        return banks[upto(s) : upto(s + 1)] if s >= 0 else []
+
+    def unit(s):
+        return [units[s]] if 0 <= s < nslot else []
+
+    quant = []
+    for s in range(LT):
+        for b in share(s):
+            head.append((b[0] + ".pe",) + b[1:])
+    slots = []
+    for s in range(nslot + LR + 1):
+        seq = []
+        mine = share(s)
+        for b in share(s + LT):
+            seq.append((b[0] + ".pe",) + b[1:])
+        if s == 5:
+            seq += [("bc.pe", 1, 0), ("bc.pe", 1, 1), ("cols.pe",)]
+        for u in unit(s):
+            seq += [("a.pe",) + u + (0,), ("a.pe",) + u + (1,)]
+        for u in unit(s - 1):
+            seq.append(("a.mean",) + u)
+        for u in unit(s - LR):
+            seq += [("a.rstd",) + u, ("a.norm",) + u]
+        if s == 5:
+            seq += [("bc.ev", 1, 0), ("bc.ev", 1, 1), ("cols.ev",)]
+        for u in unit(s):
+            seq += [("a.add",) + u + (0,), ("a.add",) + u + (1,)]
+        seq += quant
+        quant = []
+        if mine:
+            seq.append((mine[0][0] + ".ev",) + mine[0][1:])
+        for u in unit(s - LS):
+            seq.append(("a.sq",) + u)
+        for b in mine[1:]:
+            seq.append((b[0] + ".ev",) + b[1:])
+        for u in unit(s - LS):
+            seq.append(("a.std",) + u)
+        for b in mine:
+            if b[0] == "w" and b[2] % 4 == 3:
+                quant += [("w.q", b[1], b[2] // 4, 0), ("w.q", b[1], b[2] // 4, 1)]
+            if b[0] == "x" and b[1] % 2 == 1:
+                quant.append(("x.q", b[1] // 2))
+        slots.append(seq)
+    halves = [(i0, g) for (i0, ntl) in GROUPS for g in range(2)]
+    nh = len(halves)
+    cycles = []
+    for c in range(nh + SADD + 1):
+        seq = []
+        if c < nh:
+            (i0, g) = halves[c]
+            for t in range(4):
+                for br in (3, 1):
+                    seq.append(("b.pe", br, i0, 4 * g + t))
+        if 0 <= c - SPE < NT:
+            seq += [("s.pe", c - SPE, 0), ("s.pe", c - SPE, 1)]
+        if c < nh:
+            (i0, g) = halves[c]
+            for t in range(4):
+                for br in (3, 1):
+                    seq.append(("b.aff", br, i0, 4 * g + t))
+        if 1 <= c <= nh:
+            seq.append(("f.gate",) + halves[c - 1])
+        if 0 <= c - SADD < NT:
+            seq.append(("s.add", c - SADD, 0))
+        if 1 <= c <= nh:
+            seq.append(("f.q",) + halves[c - 1])
+        if 0 <= c - SADD < NT:
+            seq += [("s.add", c - SADD, 1), ("s.st", c - SADD)]
+        cycles.append(seq)
+    out = list(head)
+    for s in range(len(slots)):
+        out += slots[s]
+        if 0 <= s - B0 < len(cycles):
+            out += cycles[s - B0]
+    for c in range(max(0, len(slots) - B0), len(cycles)):
+        out += cycles[c]
+    return out
 
 
 def tile_polymlp_skiplora_pa_kernel(
@@ -64,16 +127,13 @@ def tile_polymlp_skiplora_pa_kernel(
     nc = tc.nc
     with ExitStack() as ctx:
         const = ctx.enter_context(tc.tile_pool(name="const", bufs=1))
-        rawp = ctx.enter_context(tc.tile_pool(name="rawp", bufs=12))
+        big = ctx.enter_context(tc.tile_pool(name="big", bufs=NBIG))
         browp = ctx.enter_context(tc.tile_pool(name="browp", bufs=2))
         grp = ctx.enter_context(tc.tile_pool(name="grp", bufs=2))
         vnp = ctx.enter_context(tc.tile_pool(name="vnp", bufs=1))
-        stat = ctx.enter_context(tc.tile_pool(name="stat", bufs=4))
+        stat = ctx.enter_context(tc.tile_pool(name="stat", bufs=8))
         junkp = ctx.enter_context(tc.tile_pool(name="junkp", bufs=1))
-        op = ctx.enter_context(tc.tile_pool(name="op", bufs=2))
-        otp = ctx.enter_context(tc.tile_pool(name="otp", bufs=2))
-        pmm = ctx.enter_context(tc.psum_pool(name="pmm", bufs=4))
-        ptp = ctx.enter_context(tc.psum_pool(name="ptp", bufs=4))
+        psum = ctx.enter_context(tc.psum_pool(name="psum", bufs=8))
         if PINNED:
             ctx.enter_context(tc.manual_schedule())
 
@@ -106,7 +166,7 @@ def tile_polymlp_skiplora_pa_kernel(
             return brow
 
         def load_raw(src, nm, split):
-            t = rawp.tile([P, 2 * D], BF16, tag="raw", name=nm)
+            t = big.tile([P, 2 * D], BF16, tag="k4", name=nm, align_bytes=64)
             if split:
                 nc.sync.dma_start(out=t[:].rearrange("p (j h) -> p j h", j=2), in_=src)
             else:
@@ -148,14 +208,11 @@ def tile_polymlp_skiplora_pa_kernel(
         b3p = const.tile([P, 8], F32)
         wsrc = {"U": (u1raw, u1q, u1s), "C": (craw, cq, cs)}
 
-        ops = []
+        ops = {}
         live = {}
 
-        def at(pos, lag, fn):
-            ops.append((pos + lag, len(ops), fn))
-
         def word_transposes(raw, half, nm):
-            bank = ptp.tile([P, 512], F32, tag="tp", name=nm)
+            bank = psum.tile([P, 512], F32, tag="bank", name=nm)
             words = raw[:].bitcast(F32)
             for c in range(4):
                 nc.tensor.transpose(
@@ -171,11 +228,9 @@ def tile_polymlp_skiplora_pa_kernel(
             else:
                 nc.vector.tensor_copy(out=dst, in_=src)
 
-        def unit_zu(pos, k):
-            lag = LAGS["ZU"]
-
+        def unit_zu(k):
             def pe():
-                pb = ptp.tile([P, D], BF16, tag="tp", name="pb%d" % k)
+                pb = psum.tile([P, D], BF16, tag="bank", name="pb%d" % k)
                 live["pb", k] = pb
                 for m in range(8):
                     raw = u3raw if m < 4 else z2raw
@@ -187,14 +242,12 @@ def tile_polymlp_skiplora_pa_kernel(
             def ev():
                 nc.scalar.copy(out=zuT[:, k * D : (k + 1) * D], in_=live["pb", k][:])
 
-            at(pos, lag[0], pe)
-            at(pos, lag[1], ev)
+            ops["zu.pe", k] = pe
+            ops["zu.ev", k] = ev
 
-        def unit_bc(pos, br):
-            lag = LAGS["BC"]
-
+        def unit_bc(br):
             def pe(hf):
-                ps = pmm.tile([P, 512], F32, tag="mm", name="bps%d%d" % (br, hf))
+                ps = psum.tile([P, 512], F32, tag="bank", name="bps%d%d" % (br, hf))
                 live["bps", br, hf] = ps
                 nc.tensor.matmul(
                     out=ps[:], lhsT=ones[:], rhs=brows[br][:, hf * 512 : (hf + 1) * 512], start=True, stop=True
@@ -207,11 +260,10 @@ def tile_polymlp_skiplora_pa_kernel(
                 )
 
             for hf in range(2):
-                at(pos, lag[0], lambda hf=hf: pe(hf))
-                at(pos, lag[1], lambda hf=hf: ev(hf))
+                ops["bc.pe", br, hf] = lambda hf=hf: pe(hf)
+                ops["bc.ev", br, hf] = lambda hf=hf: ev(hf)
 
-        def unit_w(pos, w, jt, engine):
-            lag = LAGS["W"]
+        def unit_w(w, jt, engine):
             hf = jt // 4
 
             def pe():
@@ -226,10 +278,10 @@ def tile_polymlp_skiplora_pa_kernel(
                     live["wb", w, jt][:].rearrange("p (g u r) -> p g r u", g=2, u=2),
                 )
 
-            at(pos, lag[0], pe)
-            at(pos, lag[1], ev)
+            ops["w.pe", w, jt] = pe
+            ops["w.ev", w, jt] = ev
 
-        def unit_wq(pos, w, hf):
+        def unit_wq(w, hf):
             def qz(g):
                 sl = slice(g * 1024 + hf * 512, g * 1024 + hf * 512 + 512)
                 nc.vector.quantize_mx(
@@ -238,10 +290,9 @@ def tile_polymlp_skiplora_pa_kernel(
                 )
 
             for g in range(2):
-                at(pos, LAGS["WQ"][0], lambda g=g: qz(g))
+                ops["w.q", w, hf, g] = lambda g=g: qz(g)
 
-        def unit_x(pos, i, engine):
-            lag = LAGS["X"]
+        def unit_x(i, engine):
             c = i // 2
 
             def pe():
@@ -249,27 +300,25 @@ def tile_polymlp_skiplora_pa_kernel(
 
             def ev():
                 if ("xg", c) not in live:
-                    live["xg", c] = grp.tile([P, 2048], BF16, tag="xg", name="xg%d" % c, align_bytes=64)
+                    live["xg", c] = big.tile([P, 2048], BF16, tag="k4", name="xg%d" % c, align_bytes=64)
                 xgv = live["xg", c][:].bitcast(F32).rearrange("p (j g r u) -> p j g r u", j=2, g=2, u=2)
                 copy_on(
                     engine, xgv[:, i % 2, :, :, :], live["xb", i][:].rearrange("p (g u r) -> p g r u", g=2, u=2)
                 )
 
-            at(pos, lag[0], pe)
-            at(pos, lag[1], ev)
+            ops["x.pe", i] = pe
+            ops["x.ev", i] = ev
 
-        def unit_xq(pos, c):
+        def unit_xq(c):
             def qz():
                 sl = slice(c * 512, (c + 1) * 512)
                 nc.vector.quantize_mx(out=xq[:, sl].bitcast(FP8X4), scales=xs[:, sl], in_=live["xg", c][:])
 
-            at(pos, LAGS["XQ"][0], qz)
+            ops["x.q", c] = qz
 
-        def unit_a(pos, br, i, engine):
-            lag = LAGS["A"]
-
+        def unit_a(br, i, engine):
             def pe(hf):
-                ps = pmm.tile([P, 512], F32, tag="mm", name="ps%d_%d_%d" % (br, i, hf))
+                ps = psum.tile([P, 512], F32, tag="bank", name="ps%d_%d_%d" % (br, i, hf))
                 live["ps", br, i, hf] = ps
                 if br == 3:
                     zc = (i // 4) * D + 512 + (i % 4) * P
@@ -309,13 +358,18 @@ def tile_polymlp_skiplora_pa_kernel(
             def squares():
                 junk = junkp.tile([P, D], BF16, tag="junk", name="junk%d_%d" % (br, i))
                 sq = stat.tile([P, 1], F32, tag="sq", name="sq%d_%d" % (br, i))
+                live["sq", br, i] = sq
                 nc.scalar.activation(
                     out=junk[:], in_=live["n", br, i][:], func=ACT.Square, bias=live["nm", br, i][:, 0:1],
                     scale=1.0, accum_out=sq[:, 0:1],
                 )
+
+            def std_():
                 std = stat.tile([P, 1], F32, tag="std", name="std%d_%d" % (br, i))
                 live["std", br, i] = std
-                nc.scalar.activation(out=std[:], in_=sq[:], func=ACT.Sqrt, bias=epsc[:, 0:1], scale=1.0 / D)
+                nc.scalar.activation(
+                    out=std[:], in_=live["sq", br, i][:], func=ACT.Sqrt, bias=epsc[:, 0:1], scale=1.0 / D
+                )
 
             def rstd_():
                 rstd = stat.tile([P, 1], F32, tag="rstd", name="rstd%d_%d" % (br, i))
@@ -341,16 +395,17 @@ def tile_polymlp_skiplora_pa_kernel(
                     )
 
             for hf in range(2):
-                at(pos, lag[0], lambda hf=hf: pe(hf))
-                at(pos, lag[1], lambda hf=hf: add_bias(hf))
-            for (k, fn) in enumerate((mean, squares, rstd_, normalise)):
-                at(pos, lag[2 + k], fn)
+                ops["a.pe", br, i, hf] = lambda hf=hf: pe(hf)
+                ops["a.add", br, i, hf] = lambda hf=hf: add_bias(hf)
+            ops["a.mean", br, i] = mean
+            ops["a.sq", br, i] = squares
+            ops["a.std", br, i] = std_
+            ops["a.rstd", br, i] = rstd_
+            ops["a.norm", br, i] = normalise
 
-        def unit_cols(pos):
-            lag = LAGS["COLS"]
-
+        def unit_cols():
             def pe():
-                pv = ptp.tile([P, 512], F32, tag="tp", name="pv")
+                pv = psum.tile([P, 512], F32, tag="bank", name="pv")
                 live["pv"] = pv
                 nc.tensor.transpose(out=pv[:, 0:P], in_=vrows[:], identity=identF[:])
 
@@ -367,16 +422,15 @@ def tile_polymlp_skiplora_pa_kernel(
                     out=b3p[:], in0=cols[:, 24:32], scalar1=al[:, 0:1], scalar2=1.0, op0=ALU.mult, op1=ALU.add
                 )
 
-            at(pos, lag[0], pe)
-            at(pos, lag[1], ev)
+            ops["cols.pe",] = pe
+            ops["cols.ev",] = ev
 
-        def unit_b(pos, i0, ntl, g, t, engine):
-            lag = LAGS["B"]
+        def unit_b(i0, ntl, g, t, engine):
             jt = 4 * g + t
             tg = ntl * P
 
             def pe(br):
-                bank = ptp.tile([P, 512], F32, tag="tp", name="nb%d_%d_%d" % (br, i0, jt))
+                bank = psum.tile([P, 512], F32, tag="bank", name="nb%d_%d_%d" % (br, i0, jt))
                 live["nb", br, i0, jt] = bank
                 for il in range(ntl):
                     nc.tensor.transpose(
@@ -387,7 +441,7 @@ def tile_polymlp_skiplora_pa_kernel(
 
             def affine(br):
                 if ("o", br, i0, g) not in live:
-                    live["o", br, i0, g] = op.tile([P, 4, tg], F32, tag="o%d" % br, name="o%d_%d_%d" % (br, i0, g))
+                    live["o", br, i0, g] = big.tile([P, 4, tg], F32, tag="k4", name="o%d_%d_%d" % (br, i0, g), align_bytes=64)
                 gcol = cols[:, jt : jt + 1] if br == 1 else g3p[:, jt : jt + 1]
                 bcol = cols[:, 8 + jt : 9 + jt] if br == 1 else b3p[:, jt : jt + 1]
                 dst = live["o", br, i0, g][:, t, :]
@@ -398,11 +452,10 @@ def tile_polymlp_skiplora_pa_kernel(
                     nc.vector.tensor_scalar(out=dst, in0=src, scalar1=gcol, scalar2=bcol, op0=ALU.mult, op1=ALU.add)
 
             for br in (3, 1):
-                at(pos, lag[0], lambda br=br: pe(br))
-                at(pos, lag[1], lambda br=br: affine(br))
+                ops["b.pe", br, i0, jt] = lambda br=br: pe(br)
+                ops["b.aff", br, i0, jt] = lambda br=br: affine(br)
 
-        def unit_f(pos, i0, ntl, g):
-            lag = LAGS["F"]
+        def unit_f(i0, ntl, g):
             tg = ntl * P
 
             def gate():
@@ -419,14 +472,12 @@ def tile_polymlp_skiplora_pa_kernel(
                 sl = slice(g * 1024 + i0 * P, g * 1024 + i0 * P + tg)
                 nc.vector.quantize_mx(out=hq[:, sl].bitcast(FP8X4), scales=hs[:, sl], in_=live["hg", i0, g][:])
 
-            at(pos, lag[0], gate)
-            at(pos, lag[1], qz)
+            ops["f.gate", i0, g] = gate
+            ops["f.q", i0, g] = qz
 
-        def unit_s(pos, i):
-            lag = LAGS["S"]
-
+        def unit_s(i):
             def pe(hf):
-                ps = pmm.tile([P, 512], F32, tag="mm", name="ps2_%d_%d" % (i, hf))
+                ps = psum.tile([P, 512], F32, tag="bank", name="ps2_%d_%d" % (i, hf))
                 live["ps2", i, hf] = ps
                 for g in range(2):
                     ls = slice(g * 1024 + i * P, g * 1024 + (i + 1) * P)
@@ -439,7 +490,7 @@ def tile_polymlp_skiplora_pa_kernel(
 
             def add_bias(hf):
                 if ("ot", i) not in live:
-                    live["ot", i] = otp.tile([P, D], F32, tag="ot", name="ot%d" % i)
+                    live["ot", i] = big.tile([P, D], F32, tag="k4", name="ot%d" % i, align_bytes=64)
                 sl = slice(hf * 512, (hf + 1) * 512)
                 nc.vector.tensor_tensor(
                     out=live["ot", i][:, sl], in0=live["ps2", i, hf][:], in1=bcc[:, sl], op=ALU.add
@@ -449,15 +500,31 @@ def tile_polymlp_skiplora_pa_kernel(
                 nc.sync.dma_start(out=o_v[:, i, :], in_=live["ot", i][:])
 
             for hf in range(2):
-                at(pos, lag[0], lambda hf=hf: pe(hf))
-                at(pos, lag[1], lambda hf=hf: add_bias(hf))
-            at(pos, lag[2], store)
+                ops["s.pe", i, hf] = lambda hf=hf: pe(hf)
+                ops["s.add", i, hf] = lambda hf=hf: add_bias(hf)
+            ops["s.st", i] = store
 
-        builders = {
-            "ZU": unit_zu, "BC": unit_bc, "W": unit_w, "WQ": unit_wq, "X": unit_x, "XQ": unit_xq,
-            "A": unit_a, "COLS": unit_cols, "B": unit_b, "F": unit_f, "S": unit_s,
-        }
-        for pos, unit in enumerate(PROGRAM):
-            builders[unit[0]](pos, *unit[1:])
-        for seq in ORDER:
-            ops[seq][2]()
+        for k in range(2):
+            unit_zu(k)
+        for br in (3, 1):
+            unit_bc(br)
+            for i in range(NT):
+                unit_a(br, i, NORM_ENGINE.get((br, i), "pool"))
+        for w in ("U", "C"):
+            for jt in range(8):
+                unit_w(w, jt, "dve" if (w, jt) in EVD else "act")
+            for hf in range(2):
+                unit_wq(w, hf)
+        for i in range(NT):
+            unit_x(i, "dve" if ("X", i) in EVD else "act")
+            unit_s(i)
+        for c in range(4):
+            unit_xq(c)
+        unit_cols()
+        for (k, (i0, ntl)) in enumerate(GROUPS):
+            for g in range(2):
+                for t in range(4):
+                    unit_b(i0, ntl, g, t, "dve" if t >= 4 - NDVE[2 * k + g] else "act")
+                unit_f(i0, ntl, g)
+        for name in plan():
+            ops[name]()

@@ -19,7 +19,7 @@ FLOPS = 2 * 1024 * (1024 * 1024 * 2 + 128 * 1024)
 PINNED = True
 NBIG = 20
 GROUPS = ((0, 2), (2, 2), (4, 2), (6, 2))
-NORM_ENGINE = {}
+NORM_ENGINE = {(1, 5): "dve"}
 LT = 1
 LS = 3
 LR = 4
@@ -27,14 +27,22 @@ FAST = 10
 B0 = 15
 SPE = 3
 SADD = 3
-NDVE = (0, 2, 2, 0, 0, 0, 0, 0)
-EVD = (("C", 6),)
+NDVE = (0, 4, 0, 0, 0, 0, 0, 0)
+EVD = (("C", 7), ("U", 1))
+GPOOL = (0, 0, 0, 0, 0, 0, 0, 0)
+MEAN_ON_ACT = False
+MEAN_ON_POOL = True
+RSQRT = False
+BC1_ON_ACT = False
+SPLIT_ST = 8
+SBC = 5
+UNITS = tuple([(3, i) for i in range(8)] + [(1, i) for i in range(8)])
 
 
 def plan():
     head = [("zu.pe", 0), ("bc.pe", 3, 0), ("bc.pe", 3, 1), ("zu.pe", 1), ("zu.ev", 0), ("bc.ev", 3, 0),
             ("bc.ev", 3, 1), ("zu.ev", 1)]
-    units = [(3, i) for i in range(NT)] + [(1, i) for i in range(NT)]
+    units = list(UNITS)
     banks = [("w", "U", j) for j in range(8)] + [("x", i) for i in range(NT)] + [("w", "C", j) for j in range(8)]
     nslot = len(units)
 
@@ -48,24 +56,30 @@ def plan():
         return [units[s]] if 0 <= s < nslot else []
 
     quant = []
+    head.append(("a.pe",) + units[0] + (0,))
     for s in range(LT):
         for b in share(s):
             head.append((b[0] + ".pe",) + b[1:])
+    head.append(("a.pe",) + units[0] + (1,))
     slots = []
     for s in range(nslot + LR + 1):
         seq = []
         mine = share(s)
         for b in share(s + LT):
             seq.append((b[0] + ".pe",) + b[1:])
-        if s == 5:
+        if s == SBC:
             seq += [("bc.pe", 1, 0), ("bc.pe", 1, 1), ("cols.pe",)]
         for u in unit(s):
-            seq += [("a.pe",) + u + (0,), ("a.pe",) + u + (1,)]
+            if s > 0:
+                seq += [("a.pe",) + u + (0,), ("a.pe",) + u + (1,)]
         for u in unit(s - 1):
-            seq.append(("a.mean",) + u)
+            if not MEAN_ON_ACT:
+                seq.append(("a.mean",) + u)
         for u in unit(s - LR):
-            seq += [("a.rstd",) + u, ("a.norm",) + u]
-        if s == 5:
+            if not RSQRT:
+                seq.append(("a.rstd",) + u)
+            seq.append(("a.norm",) + u)
+        if s == SBC:
             seq += [("bc.ev", 1, 0), ("bc.ev", 1, 1), ("cols.ev",)]
         for u in unit(s):
             seq += [("a.add",) + u + (0,), ("a.add",) + u + (1,)]
@@ -73,6 +87,9 @@ def plan():
         quant = []
         if mine:
             seq.append((mine[0][0] + ".ev",) + mine[0][1:])
+        for u in unit(s - 1):
+            if MEAN_ON_ACT:
+                seq.append(("a.mean",) + u)
         for u in unit(s - LS):
             seq.append(("a.sq",) + u)
         for b in mine[1:]:
@@ -106,17 +123,24 @@ def plan():
             seq.append(("f.gate",) + halves[c - 1])
         if 0 <= c - SADD < NT:
             seq.append(("s.add", c - SADD, 0))
+            if c - SADD >= NT - SPLIT_ST:
+                seq.append(("s.sth", c - SADD, 0))
         if 1 <= c <= nh:
             seq.append(("f.q",) + halves[c - 1])
         if 0 <= c - SADD < NT:
-            seq += [("s.add", c - SADD, 1), ("s.st", c - SADD)]
+            seq.append(("s.add", c - SADD, 1))
+            seq.append(("s.sth", c - SADD, 1) if c - SADD >= NT - SPLIT_ST else ("s.st", c - SADD))
         cycles.append(seq)
     out = list(head)
+    nxt = 0
     for s in range(len(slots)):
         out += slots[s]
-        if 0 <= s - B0 < len(cycles):
-            out += cycles[s - B0]
-    for c in range(max(0, len(slots) - B0), len(cycles)):
+        if nxt < len(cycles) and s >= B0:
+            tiles = range(halves[nxt][0], halves[nxt][0] + 2) if nxt < nh else ()
+            if all(units.index((br, i)) + LR <= s for br in (1, 3) for i in tiles):
+                out += cycles[nxt]
+                nxt += 1
+    for c in range(nxt, len(cycles)):
         out += cycles[c]
     return out
 
@@ -148,9 +172,13 @@ def tile_polymlp_skiplora_pa_kernel(
         c_v = C_w.rearrange("(c j p) h -> c p j h", c=4, j=2)
 
         u3raw = const.tile([P, D], BF16)
-        nc.sync.dma_start(out=u3raw[:].rearrange("p (a w) -> p a w", a=4), in_=u3_v)
         z2raw = const.tile([P, D], BF16)
-        nc.sync.dma_start(out=z2raw[:], in_=z_v)
+        for k in range(2):
+            nc.sync.dma_start(
+                out=u3raw[:, k * 512 : (k + 1) * 512].rearrange("p (a w) -> p a w", a=2),
+                in_=u3_v[:, 2 * k : 2 * k + 2, :],
+            )
+            nc.sync.dma_start(out=z2raw[:, k * 512 : (k + 1) * 512], in_=z_v[:, k * 512 : (k + 1) * 512])
 
         identB = const.tile([P, P], BF16)
         make_identity(nc, identB[:])
@@ -177,7 +205,7 @@ def tile_polymlp_skiplora_pa_kernel(
         epsc = const.tile([P, 1], F32)
         nc.vector.memset(epsc[:], EPS)
         warm = const.tile([P, 1], F32)
-        nc.scalar.activation(out=warm[:], in_=epsc[:], func=ACT.Sqrt)
+        nc.scalar.activation(out=warm[:], in_=epsc[:], func=(ACT.Abs_reciprocal_sqrt if RSQRT else ACT.Sqrt))
         vrows = const.tile([P, P], F32)
         nc.vector.memset(vrows[:], 0.0)
         u1raw = [load_raw(u1_v[a], "u1raw%d" % a, False) for a in range(4)]
@@ -254,9 +282,10 @@ def tile_polymlp_skiplora_pa_kernel(
                 )
 
             def ev(hf):
-                nc.vector.tensor_copy(
-                    out=bcs[br][:, hf * 512 : (hf + 1) * 512].rearrange("p (a e r) -> p a e r", a=2, e=2),
-                    in_=live["bps", br, hf][:].rearrange("p (a r e) -> p a e r", a=2, e=2),
+                copy_on(
+                    "act" if (br == 1 and BC1_ON_ACT) else "dve",
+                    bcs[br][:, hf * 512 : (hf + 1) * 512].rearrange("p (a e r) -> p a e r", a=2, e=2),
+                    live["bps", br, hf][:].rearrange("p (a r e) -> p a e r", a=2, e=2),
                 )
 
             for hf in range(2):
@@ -350,10 +379,17 @@ def tile_polymlp_skiplora_pa_kernel(
                 negmean = stat.tile([P, 1], F32, tag="negmean", name="negmean%d_%d" % (br, i))
                 live["nm", br, i] = negmean
                 ssum = live["ssum", br, i]
-                nc.vector.tensor_scalar(
-                    out=negmean[:], in0=ssum[:, 0:1], scalar1=ssum[:, 1:2], scalar2=-1.0 / D,
-                    op0=ALU.add, op1=ALU.mult,
-                )
+                if MEAN_ON_ACT:
+                    scr = stat.tile([P, 2], F32, tag="scr", name="scr%d_%d" % (br, i))
+                    nc.scalar.activation(
+                        out=scr[:], in_=ssum[:], func=ACT.Identity, scale=-1.0 / D, accum_out=negmean[:, 0:1]
+                    )
+                else:
+                    eng = nc.gpsimd if MEAN_ON_POOL else nc.vector
+                    eng.tensor_scalar(
+                        out=negmean[:], in0=ssum[:, 0:1], scalar1=ssum[:, 1:2], scalar2=-1.0 / D,
+                        op0=ALU.add, op1=ALU.mult,
+                    )
 
             def squares():
                 junk = junkp.tile([P, D], BF16, tag="junk", name="junk%d_%d" % (br, i))
@@ -365,11 +401,19 @@ def tile_polymlp_skiplora_pa_kernel(
                 )
 
             def std_():
-                std = stat.tile([P, 1], F32, tag="std", name="std%d_%d" % (br, i))
-                live["std", br, i] = std
-                nc.scalar.activation(
-                    out=std[:], in_=live["sq", br, i][:], func=ACT.Sqrt, bias=epsc[:, 0:1], scale=1.0 / D
-                )
+                if RSQRT:
+                    rstd = stat.tile([P, 1], F32, tag="rstd", name="rstd%d_%d" % (br, i))
+                    live["rstd", br, i] = rstd
+                    nc.scalar.activation(
+                        out=rstd[:], in_=live["sq", br, i][:], func=ACT.Abs_reciprocal_sqrt, bias=epsc[:, 0:1],
+                        scale=1.0 / D,
+                    )
+                else:
+                    std = stat.tile([P, 1], F32, tag="std", name="std%d_%d" % (br, i))
+                    live["std", br, i] = std
+                    nc.scalar.activation(
+                        out=std[:], in_=live["sq", br, i][:], func=ACT.Sqrt, bias=epsc[:, 0:1], scale=1.0 / D
+                    )
 
             def rstd_():
                 rstd = stat.tile([P, 1], F32, tag="rstd", name="rstd%d_%d" % (br, i))
@@ -455,13 +499,14 @@ def tile_polymlp_skiplora_pa_kernel(
                 ops["b.pe", br, i0, jt] = lambda br=br: pe(br)
                 ops["b.aff", br, i0, jt] = lambda br=br: affine(br)
 
-        def unit_f(i0, ntl, g):
+        def unit_f(i0, ntl, g, engine):
             tg = ntl * P
 
             def gate():
                 hg = grp.tile([P, 4 * tg], BF16, tag="hg", name="hg%d_%d" % (i0, g), align_bytes=64)
                 live["hg", i0, g] = hg
-                nc.vector.tensor_tensor(
+                eng = nc.gpsimd if engine == "pool" else nc.vector
+                eng.tensor_tensor(
                     out=hg[:].rearrange("p (c i t) -> p c t i", i=4, t=4),
                     in0=live["o", 1, i0, g][:].rearrange("p t (c i) -> p c t i", i=4),
                     in1=live["o", 3, i0, g][:].rearrange("p t (c i) -> p c t i", i=4),
@@ -499,10 +544,16 @@ def tile_polymlp_skiplora_pa_kernel(
             def store():
                 nc.sync.dma_start(out=o_v[:, i, :], in_=live["ot", i][:])
 
+            def store_half(hf):
+                sl = slice(hf * 512, (hf + 1) * 512)
+                nc.sync.dma_start(out=o_v[:, i, sl], in_=live["ot", i][:, sl])
+
             for hf in range(2):
                 ops["s.pe", i, hf] = lambda hf=hf: pe(hf)
                 ops["s.add", i, hf] = lambda hf=hf: add_bias(hf)
             ops["s.st", i] = store
+            for hf in range(2):
+                ops["s.sth", i, hf] = lambda hf=hf: store_half(hf)
 
         for k in range(2):
             unit_zu(k)
@@ -525,6 +576,6 @@ def tile_polymlp_skiplora_pa_kernel(
             for g in range(2):
                 for t in range(4):
                     unit_b(i0, ntl, g, t, "dve" if t >= 4 - NDVE[2 * k + g] else "act")
-                unit_f(i0, ntl, g)
+                unit_f(i0, ntl, g, "pool" if GPOOL[2 * k + g] else "dve")
         for name in plan():
             ops[name]()

@@ -16,7 +16,7 @@ NT = 8
 D = 1024
 EPS = 1e-6
 FLOPS = 2 * 1024 * (1024 * 1024 * 2 + 128 * 1024)
-PINNED = True
+PINNED = False
 NBIG = 20
 GROUPS = ((0, 2), (2, 2), (4, 2), (6, 2))
 NORM_ENGINE = {(1, 5): "dve"}

@@ -14,135 +14,34 @@ ACT = mybir.ActivationFunctionType
 P = 128
 NT = 8
 D = 1024
+BANK = 512
 EPS = 1e-6
 FLOPS = 2 * 1024 * (1024 * 1024 * 2 + 128 * 1024)
-PINNED = False
-NBIG = 20
-GROUPS = ((0, 2), (2, 2), (4, 2), (6, 2))
-NORM_ENGINE = {(1, 5): "dve"}
-LT = 1
-LS = 3
-LR = 4
-FAST = 10
-B0 = 15
-SPE = 3
-SADD = 3
-NDVE = (0, 4, 0, 0, 0, 0, 0, 0)
-EVD = (("C", 7), ("U", 1))
-GPOOL = (0, 0, 0, 0, 0, 0, 0, 0)
-MEAN_ON_ACT = False
-MEAN_ON_POOL = True
-RSQRT = False
-BC1_ON_ACT = False
-SPLIT_ST = 8
-SBC = 5
-UNITS = tuple([(3, i) for i in range(8)] + [(1, i) for i in range(8)])
+
+UNITS = tuple([(3, i) for i in range(NT)] + [(1, i) for i in range(NT)])
+WORD_BANKS = tuple([("U", j) for j in range(8)] + [("x", i) for i in range(NT)] + [("C", j) for j in range(8)])
+SLOTS_4K = 20
+
+LAG_MEAN = 1
+LAG_SQUARES = 3
+LAG_NORMALISE = 4
+FAST_SLOTS = 10
+SLOT_BIAS1 = 5
+N_CYCLES = 8
+LAG_STAGE2 = 3
+FIRST_CYCLE_SLOT = 15
+CYCLE_ON_VECTOR = 1
 
 
-def plan():
-    head = [("zu.pe", 0), ("bc.pe", 3, 0), ("bc.pe", 3, 1), ("zu.pe", 1), ("zu.ev", 0), ("bc.ev", 3, 0),
-            ("bc.ev", 3, 1), ("zu.ev", 1)]
-    units = list(UNITS)
-    banks = [("w", "U", j) for j in range(8)] + [("x", i) for i in range(NT)] + [("w", "C", j) for j in range(8)]
-    nslot = len(units)
+def word_banks_of_slot(s):
+    def upto(n):
+        return min(len(WORD_BANKS), 2 * n if n <= FAST_SLOTS else FAST_SLOTS + n)
 
-    def upto(s):
-        return min(len(banks), 2 * s if s <= FAST else 2 * FAST + (s - FAST))
+    return WORD_BANKS[upto(s) : upto(s + 1)] if s >= 0 else ()
 
-    def share(s):
-        return banks[upto(s) : upto(s + 1)] if s >= 0 else []
 
-    def unit(s):
-        return [units[s]] if 0 <= s < nslot else []
-
-    quant = []
-    head.append(("a.pe",) + units[0] + (0,))
-    for s in range(LT):
-        for b in share(s):
-            head.append((b[0] + ".pe",) + b[1:])
-    head.append(("a.pe",) + units[0] + (1,))
-    slots = []
-    for s in range(nslot + LR + 1):
-        seq = []
-        mine = share(s)
-        for b in share(s + LT):
-            seq.append((b[0] + ".pe",) + b[1:])
-        if s == SBC:
-            seq += [("bc.pe", 1, 0), ("bc.pe", 1, 1), ("cols.pe",)]
-        for u in unit(s):
-            if s > 0:
-                seq += [("a.pe",) + u + (0,), ("a.pe",) + u + (1,)]
-        for u in unit(s - 1):
-            if not MEAN_ON_ACT:
-                seq.append(("a.mean",) + u)
-        for u in unit(s - LR):
-            if not RSQRT:
-                seq.append(("a.rstd",) + u)
-            seq.append(("a.norm",) + u)
-        if s == SBC:
-            seq += [("bc.ev", 1, 0), ("bc.ev", 1, 1), ("cols.ev",)]
-        for u in unit(s):
-            seq += [("a.add",) + u + (0,), ("a.add",) + u + (1,)]
-        seq += quant
-        quant = []
-        if mine:
-            seq.append((mine[0][0] + ".ev",) + mine[0][1:])
-        for u in unit(s - 1):
-            if MEAN_ON_ACT:
-                seq.append(("a.mean",) + u)
-        for u in unit(s - LS):
-            seq.append(("a.sq",) + u)
-        for b in mine[1:]:
-            seq.append((b[0] + ".ev",) + b[1:])
-        for u in unit(s - LS):
-            seq.append(("a.std",) + u)
-        for b in mine:
-            if b[0] == "w" and b[2] % 4 == 3:
-                quant += [("w.q", b[1], b[2] // 4, 0), ("w.q", b[1], b[2] // 4, 1)]
-            if b[0] == "x" and b[1] % 2 == 1:
-                quant.append(("x.q", b[1] // 2))
-        slots.append(seq)
-    halves = [(i0, g) for (i0, ntl) in GROUPS for g in range(2)]
-    nh = len(halves)
-    cycles = []
-    for c in range(nh + SADD + 1):
-        seq = []
-        if c < nh:
-            (i0, g) = halves[c]
-            for t in range(4):
-                for br in (3, 1):
-                    seq.append(("b.pe", br, i0, 4 * g + t))
-        if 0 <= c - SPE < NT:
-            seq += [("s.pe", c - SPE, 0), ("s.pe", c - SPE, 1)]
-        if c < nh:
-            (i0, g) = halves[c]
-            for t in range(4):
-                for br in (3, 1):
-                    seq.append(("b.aff", br, i0, 4 * g + t))
-        if 1 <= c <= nh:
-            seq.append(("f.gate",) + halves[c - 1])
-        if 0 <= c - SADD < NT:
-            seq.append(("s.add", c - SADD, 0))
-            if c - SADD >= NT - SPLIT_ST:
-                seq.append(("s.sth", c - SADD, 0))
-        if 1 <= c <= nh:
-            seq.append(("f.q",) + halves[c - 1])
-        if 0 <= c - SADD < NT:
-            seq.append(("s.add", c - SADD, 1))
-            seq.append(("s.sth", c - SADD, 1) if c - SADD >= NT - SPLIT_ST else ("s.st", c - SADD))
-        cycles.append(seq)
-    out = list(head)
-    nxt = 0
-    for s in range(len(slots)):
-        out += slots[s]
-        if nxt < len(cycles) and s >= B0:
-            tiles = range(halves[nxt][0], halves[nxt][0] + 2) if nxt < nh else ()
-            if all(units.index((br, i)) + LR <= s for br in (1, 3) for i in tiles):
-                out += cycles[nxt]
-                nxt += 1
-    for c in range(nxt, len(cycles)):
-        out += cycles[c]
-    return out
+def units_of_slot(s):
+    return UNITS[s : s + 1] if s >= 0 else ()
 
 
 def tile_polymlp_skiplora_pa_kernel(
@@ -151,15 +50,13 @@ def tile_polymlp_skiplora_pa_kernel(
     nc = tc.nc
     with ExitStack() as ctx:
         const = ctx.enter_context(tc.tile_pool(name="const", bufs=1))
-        big = ctx.enter_context(tc.tile_pool(name="big", bufs=NBIG))
+        big = ctx.enter_context(tc.tile_pool(name="big", bufs=SLOTS_4K))
         browp = ctx.enter_context(tc.tile_pool(name="browp", bufs=2))
         grp = ctx.enter_context(tc.tile_pool(name="grp", bufs=2))
         vnp = ctx.enter_context(tc.tile_pool(name="vnp", bufs=1))
         stat = ctx.enter_context(tc.tile_pool(name="stat", bufs=8))
         junkp = ctx.enter_context(tc.tile_pool(name="junkp", bufs=1))
         psum = ctx.enter_context(tc.psum_pool(name="psum", bufs=8))
-        if PINNED:
-            ctx.enter_context(tc.manual_schedule())
 
         xf = x.flatten_outer_dims()
         zf = z2.flatten_outer_dims()
@@ -205,7 +102,7 @@ def tile_polymlp_skiplora_pa_kernel(
         epsc = const.tile([P, 1], F32)
         nc.vector.memset(epsc[:], EPS)
         warm = const.tile([P, 1], F32)
-        nc.scalar.activation(out=warm[:], in_=epsc[:], func=(ACT.Abs_reciprocal_sqrt if RSQRT else ACT.Sqrt))
+        nc.scalar.activation(out=warm[:], in_=epsc[:], func=ACT.Sqrt)
         vrows = const.tile([P, P], F32)
         nc.vector.memset(vrows[:], 0.0)
         u1raw = [load_raw(u1_v[a], "u1raw%d" % a, False) for a in range(4)]
@@ -234,348 +131,276 @@ def tile_polymlp_skiplora_pa_kernel(
         cols = const.tile([P, 32], F32)
         g3p = const.tile([P, 8], F32)
         b3p = const.tile([P, 8], F32)
-        wsrc = {"U": (u1raw, u1q, u1s), "C": (craw, cq, cs)}
+        raws = {"U": u1raw, "x": xraw, "C": craw}
+        packed = {"U": (u1q, u1s), "C": (cq, cs)}
 
-        ops = {}
         live = {}
 
-        def word_transposes(raw, half, nm):
-            bank = psum.tile([P, 512], F32, tag="bank", name=nm)
-            words = raw[:].bitcast(F32)
+        def small_transposes(k):
+            pb = psum.tile([P, D], BF16, tag="bank", name="pb%d" % k)
+            live["pb", k] = pb
+            for m in range(8):
+                raw = u3raw if m < 4 else z2raw
+                col = (4 * k + m % 4) * P
+                nc.tensor.transpose(out=pb[:, m * P : (m + 1) * P], in_=raw[:, col : col + P], identity=identB[:])
+
+        def small_copy(k):
+            nc.scalar.copy(out=zuT[:, k * D : (k + 1) * D], in_=live["pb", k][:])
+
+        def plane_matmul(br, hf):
+            ps = psum.tile([P, BANK], F32, tag="bank", name="bps%d%d" % (br, hf))
+            live["bps", br, hf] = ps
+            nc.tensor.matmul(
+                out=ps[:], lhsT=ones[:], rhs=brows[br][:, hf * 512 : (hf + 1) * 512], start=True, stop=True
+            )
+
+        def plane_copy(br, hf):
+            nc.vector.tensor_copy(
+                out=bcs[br][:, hf * 512 : (hf + 1) * 512].rearrange("p (a e r) -> p a e r", a=2, e=2),
+                in_=live["bps", br, hf][:].rearrange("p (a r e) -> p a e r", a=2, e=2),
+            )
+
+        def word_transposes(kind, j):
+            bank = psum.tile([P, BANK], F32, tag="bank", name="wb%s%d" % (kind, j))
+            live["wb", kind, j] = bank
+            words = raws[kind][j // 2][:].bitcast(F32)
             for c in range(4):
                 nc.tensor.transpose(
                     out=bank[:, c * P : (c + 1) * P],
-                    in_=words[:, half * 512 + c * P : half * 512 + (c + 1) * P],
+                    in_=words[:, (j % 2) * 512 + c * P : (j % 2) * 512 + (c + 1) * P],
                     identity=identF[:],
                 )
-            return bank
 
-        def copy_on(engine, dst, src):
-            if engine == "act":
-                nc.scalar.copy(out=dst, in_=src)
+        def word_copy(kind, j):
+            src = live["wb", kind, j][:].rearrange("p (g u r) -> p g r u", g=2, u=2)
+            if kind == "x":
+                if j % 2 == 0:
+                    live["xg", j // 2] = big.tile([P, 2048], BF16, tag="k4", name="xg%d" % (j // 2), align_bytes=64)
+                view = live["xg", j // 2][:].bitcast(F32).rearrange("p (j g r u) -> p j g r u", j=2, g=2, u=2)
+                nc.scalar.copy(out=view[:, j % 2, :, :, :], in_=src)
             else:
-                nc.vector.tensor_copy(out=dst, in_=src)
-
-        def unit_zu(k):
-            def pe():
-                pb = psum.tile([P, D], BF16, tag="bank", name="pb%d" % k)
-                live["pb", k] = pb
-                for m in range(8):
-                    raw = u3raw if m < 4 else z2raw
-                    col = (4 * k + m % 4) * P
-                    nc.tensor.transpose(
-                        out=pb[:, m * P : (m + 1) * P], in_=raw[:, col : col + P], identity=identB[:]
+                if j % 4 == 0:
+                    live["wg", kind, j // 4] = grp.tile(
+                        [P, 4096], BF16, tag="wg", name="wg%s%d" % (kind, j // 4), align_bytes=64
                     )
+                view = live["wg", kind, j // 4][:].bitcast(F32).rearrange("p (g j r u) -> p g j r u", g=2, j=4, u=2)
+                nc.scalar.copy(out=view[:, :, j % 4, :, :], in_=src)
 
-            def ev():
-                nc.scalar.copy(out=zuT[:, k * D : (k + 1) * D], in_=live["pb", k][:])
-
-            ops["zu.pe", k] = pe
-            ops["zu.ev", k] = ev
-
-        def unit_bc(br):
-            def pe(hf):
-                ps = psum.tile([P, 512], F32, tag="bank", name="bps%d%d" % (br, hf))
-                live["bps", br, hf] = ps
-                nc.tensor.matmul(
-                    out=ps[:], lhsT=ones[:], rhs=brows[br][:, hf * 512 : (hf + 1) * 512], start=True, stop=True
-                )
-
-            def ev(hf):
-                copy_on(
-                    "act" if (br == 1 and BC1_ON_ACT) else "dve",
-                    bcs[br][:, hf * 512 : (hf + 1) * 512].rearrange("p (a e r) -> p a e r", a=2, e=2),
-                    live["bps", br, hf][:].rearrange("p (a r e) -> p a e r", a=2, e=2),
-                )
-
-            for hf in range(2):
-                ops["bc.pe", br, hf] = lambda hf=hf: pe(hf)
-                ops["bc.ev", br, hf] = lambda hf=hf: ev(hf)
-
-        def unit_w(w, jt, engine):
-            hf = jt // 4
-
-            def pe():
-                live["wb", w, jt] = word_transposes(wsrc[w][0][jt // 2], jt % 2, "wb%s%d" % (w, jt))
-
-            def ev():
-                if ("wg", w, hf) not in live:
-                    live["wg", w, hf] = grp.tile([P, 4096], BF16, tag="wg", name="wg%s%d" % (w, hf), align_bytes=64)
-                wgv = live["wg", w, hf][:].bitcast(F32).rearrange("p (g j r u) -> p g j r u", g=2, j=4, u=2)
-                copy_on(
-                    engine, wgv[:, :, jt % 4, :, :],
-                    live["wb", w, jt][:].rearrange("p (g u r) -> p g r u", g=2, u=2),
-                )
-
-            ops["w.pe", w, jt] = pe
-            ops["w.ev", w, jt] = ev
-
-        def unit_wq(w, hf):
-            def qz(g):
-                sl = slice(g * 1024 + hf * 512, g * 1024 + hf * 512 + 512)
-                nc.vector.quantize_mx(
-                    out=wsrc[w][1][:, sl].bitcast(FP8X4), scales=wsrc[w][2][:, sl],
-                    in_=live["wg", w, hf][:, g * 2048 : (g + 1) * 2048],
-                )
-
-            for g in range(2):
-                ops["w.q", w, hf, g] = lambda g=g: qz(g)
-
-        def unit_x(i, engine):
-            c = i // 2
-
-            def pe():
-                live["xb", i] = word_transposes(xraw[c], i % 2, "xb%d" % i)
-
-            def ev():
-                if ("xg", c) not in live:
-                    live["xg", c] = big.tile([P, 2048], BF16, tag="k4", name="xg%d" % c, align_bytes=64)
-                xgv = live["xg", c][:].bitcast(F32).rearrange("p (j g r u) -> p j g r u", j=2, g=2, u=2)
-                copy_on(
-                    engine, xgv[:, i % 2, :, :, :], live["xb", i][:].rearrange("p (g u r) -> p g r u", g=2, u=2)
-                )
-
-            ops["x.pe", i] = pe
-            ops["x.ev", i] = ev
-
-        def unit_xq(c):
-            def qz():
-                sl = slice(c * 512, (c + 1) * 512)
-                nc.vector.quantize_mx(out=xq[:, sl].bitcast(FP8X4), scales=xs[:, sl], in_=live["xg", c][:])
-
-            ops["x.q", c] = qz
-
-        def unit_a(br, i, engine):
-            def pe(hf):
-                ps = psum.tile([P, 512], F32, tag="bank", name="ps%d_%d_%d" % (br, i, hf))
-                live["ps", br, i, hf] = ps
-                if br == 3:
-                    zc = (i // 4) * D + 512 + (i % 4) * P
-                    nc.tensor.matmul(
-                        out=ps[:], lhsT=zuT[:, zc : zc + P], rhs=zuT[:, hf * D : hf * D + 512],
-                        start=True, stop=True,
-                    )
-                else:
-                    for g in range(2):
-                        ls = slice(i * 256 + g * P, i * 256 + (g + 1) * P)
-                        rs = slice(g * 1024 + hf * 512, g * 1024 + hf * 512 + 512)
-                        nc.tensor.matmul_mx(
-                            out=ps[:], lhsT=xq[:, ls].bitcast(FP8X4), lhsT_scale=xs[:, ls],
-                            rhs=u1q[:, rs].bitcast(FP8X4), rhs_scale=u1s[:, rs],
-                            start=(g == 0), stop=(g == 1),
-                        )
-
-            def add_bias(hf):
-                if ("n", br, i) not in live:
-                    live["n", br, i] = vnp.tile([P, D], F32, name="n%d_%d" % (br, i))
-                    live["ssum", br, i] = stat.tile([P, 2], F32, tag="ssum", name="ssum%d_%d" % (br, i))
-                sl = slice(hf * 512, (hf + 1) * 512)
-                nc.vector.scalar_tensor_tensor(
-                    out=live["n", br, i][:, sl], in0=live["ps", br, i, hf][:], scalar=1.0, in1=bcs[br][:, sl],
-                    op0=ALU.mult, op1=ALU.add, accum_out=live["ssum", br, i][:, hf : hf + 1],
-                )
-
-            def mean():
-                negmean = stat.tile([P, 1], F32, tag="negmean", name="negmean%d_%d" % (br, i))
-                live["nm", br, i] = negmean
-                ssum = live["ssum", br, i]
-                if MEAN_ON_ACT:
-                    scr = stat.tile([P, 2], F32, tag="scr", name="scr%d_%d" % (br, i))
-                    nc.scalar.activation(
-                        out=scr[:], in_=ssum[:], func=ACT.Identity, scale=-1.0 / D, accum_out=negmean[:, 0:1]
-                    )
-                else:
-                    eng = nc.gpsimd if MEAN_ON_POOL else nc.vector
-                    eng.tensor_scalar(
-                        out=negmean[:], in0=ssum[:, 0:1], scalar1=ssum[:, 1:2], scalar2=-1.0 / D,
-                        op0=ALU.add, op1=ALU.mult,
-                    )
-
-            def squares():
-                junk = junkp.tile([P, D], BF16, tag="junk", name="junk%d_%d" % (br, i))
-                sq = stat.tile([P, 1], F32, tag="sq", name="sq%d_%d" % (br, i))
-                live["sq", br, i] = sq
-                nc.scalar.activation(
-                    out=junk[:], in_=live["n", br, i][:], func=ACT.Square, bias=live["nm", br, i][:, 0:1],
-                    scale=1.0, accum_out=sq[:, 0:1],
-                )
-
-            def std_():
-                if RSQRT:
-                    rstd = stat.tile([P, 1], F32, tag="rstd", name="rstd%d_%d" % (br, i))
-                    live["rstd", br, i] = rstd
-                    nc.scalar.activation(
-                        out=rstd[:], in_=live["sq", br, i][:], func=ACT.Abs_reciprocal_sqrt, bias=epsc[:, 0:1],
-                        scale=1.0 / D,
-                    )
-                else:
-                    std = stat.tile([P, 1], F32, tag="std", name="std%d_%d" % (br, i))
-                    live["std", br, i] = std
-                    nc.scalar.activation(
-                        out=std[:], in_=live["sq", br, i][:], func=ACT.Sqrt, bias=epsc[:, 0:1], scale=1.0 / D
-                    )
-
-            def rstd_():
-                rstd = stat.tile([P, 1], F32, tag="rstd", name="rstd%d_%d" % (br, i))
-                live["rstd", br, i] = rstd
-                nc.vector.reciprocal(out=rstd[:], in_=live["std", br, i][:])
-                if engine == "act":
-                    nmr = stat.tile([P, 1], F32, tag="nmr", name="nmr%d_%d" % (br, i))
-                    live["nmr", br, i] = nmr
-                    nc.vector.tensor_tensor(out=nmr[:], in0=live["nm", br, i][:], in1=rstd[:], op=ALU.mult)
-
-            def normalise():
-                v = live["n", br, i]
-                if engine == "act":
-                    nc.scalar.activation(
-                        out=v[:], in_=v[:], func=ACT.Identity, bias=live["nmr", br, i][:, 0:1],
-                        scale=live["rstd", br, i][:, 0:1],
-                    )
-                else:
-                    eng = nc.gpsimd if engine == "pool" else nc.vector
-                    eng.tensor_scalar(
-                        out=v[:], in0=v[:], scalar1=live["nm", br, i][:, 0:1], scalar2=live["rstd", br, i][:, 0:1],
-                        op0=ALU.add, op1=ALU.mult,
-                    )
-
-            for hf in range(2):
-                ops["a.pe", br, i, hf] = lambda hf=hf: pe(hf)
-                ops["a.add", br, i, hf] = lambda hf=hf: add_bias(hf)
-            ops["a.mean", br, i] = mean
-            ops["a.sq", br, i] = squares
-            ops["a.std", br, i] = std_
-            ops["a.rstd", br, i] = rstd_
-            ops["a.norm", br, i] = normalise
-
-        def unit_cols():
-            def pe():
-                pv = psum.tile([P, 512], F32, tag="bank", name="pv")
-                live["pv"] = pv
-                nc.tensor.transpose(out=pv[:, 0:P], in_=vrows[:], identity=identF[:])
-
-            def ev():
-                vw = const.tile([P, 16], F32, name="vw")
-                nc.vector.tensor_copy(out=vw[:], in_=live["pv"][:, 0:16])
-                nc.vector.tensor_copy(out=cols[:], in_=vw[:].bitcast(BF16))
-                al = const.tile([P, 1], F32, name="al")
-                nc.vector.tensor_copy(out=al[:], in_=al_bf[:])
-                nc.vector.tensor_scalar(
-                    out=g3p[:], in0=cols[:, 16:24], scalar1=al[:, 0:1], scalar2=None, op0=ALU.mult
-                )
-                nc.vector.tensor_scalar(
-                    out=b3p[:], in0=cols[:, 24:32], scalar1=al[:, 0:1], scalar2=1.0, op0=ALU.mult, op1=ALU.add
-                )
-
-            ops["cols.pe",] = pe
-            ops["cols.ev",] = ev
-
-        def unit_b(i0, ntl, g, t, engine):
-            jt = 4 * g + t
-            tg = ntl * P
-
-            def pe(br):
-                bank = psum.tile([P, 512], F32, tag="bank", name="nb%d_%d_%d" % (br, i0, jt))
-                live["nb", br, i0, jt] = bank
-                for il in range(ntl):
-                    nc.tensor.transpose(
-                        out=bank[:, il * P : (il + 1) * P],
-                        in_=live["n", br, i0 + il][:, jt * P : (jt + 1) * P],
-                        identity=identF[:],
-                    )
-
-            def affine(br):
-                if ("o", br, i0, g) not in live:
-                    live["o", br, i0, g] = big.tile([P, 4, tg], F32, tag="k4", name="o%d_%d_%d" % (br, i0, g), align_bytes=64)
-                gcol = cols[:, jt : jt + 1] if br == 1 else g3p[:, jt : jt + 1]
-                bcol = cols[:, 8 + jt : 9 + jt] if br == 1 else b3p[:, jt : jt + 1]
-                dst = live["o", br, i0, g][:, t, :]
-                src = live["nb", br, i0, jt][:, 0:tg]
-                if engine == "act":
-                    nc.scalar.activation(out=dst, in_=src, func=ACT.Identity, bias=bcol, scale=gcol)
-                else:
-                    nc.vector.tensor_scalar(out=dst, in0=src, scalar1=gcol, scalar2=bcol, op0=ALU.mult, op1=ALU.add)
-
-            for br in (3, 1):
-                ops["b.pe", br, i0, jt] = lambda br=br: pe(br)
-                ops["b.aff", br, i0, jt] = lambda br=br: affine(br)
-
-        def unit_f(i0, ntl, g, engine):
-            tg = ntl * P
-
-            def gate():
-                hg = grp.tile([P, 4 * tg], BF16, tag="hg", name="hg%d_%d" % (i0, g), align_bytes=64)
-                live["hg", i0, g] = hg
-                eng = nc.gpsimd if engine == "pool" else nc.vector
-                eng.tensor_tensor(
-                    out=hg[:].rearrange("p (c i t) -> p c t i", i=4, t=4),
-                    in0=live["o", 1, i0, g][:].rearrange("p t (c i) -> p c t i", i=4),
-                    in1=live["o", 3, i0, g][:].rearrange("p t (c i) -> p c t i", i=4),
-                    op=ALU.mult,
-                )
-
-            def qz():
-                sl = slice(g * 1024 + i0 * P, g * 1024 + i0 * P + tg)
-                nc.vector.quantize_mx(out=hq[:, sl].bitcast(FP8X4), scales=hs[:, sl], in_=live["hg", i0, g][:])
-
-            ops["f.gate", i0, g] = gate
-            ops["f.q", i0, g] = qz
-
-        def unit_s(i):
-            def pe(hf):
-                ps = psum.tile([P, 512], F32, tag="bank", name="ps2_%d_%d" % (i, hf))
-                live["ps2", i, hf] = ps
+        def quantise_if_complete(kind, j):
+            if kind == "x" and j % 2 == 1:
+                sl = slice((j // 2) * 512, (j // 2 + 1) * 512)
+                nc.vector.quantize_mx(out=xq[:, sl].bitcast(FP8X4), scales=xs[:, sl], in_=live["xg", j // 2][:])
+            if kind != "x" and j % 4 == 3:
+                (codes, scales) = packed[kind]
                 for g in range(2):
-                    ls = slice(g * 1024 + i * P, g * 1024 + (i + 1) * P)
+                    sl = slice(g * 1024 + (j // 4) * 512, g * 1024 + (j // 4) * 512 + 512)
+                    nc.vector.quantize_mx(
+                        out=codes[:, sl].bitcast(FP8X4), scales=scales[:, sl],
+                        in_=live["wg", kind, j // 4][:, g * 2048 : (g + 1) * 2048],
+                    )
+
+        def unit_matmul(br, i, hf):
+            ps = psum.tile([P, BANK], F32, tag="bank", name="ps%d_%d_%d" % (br, i, hf))
+            live["ps", br, i, hf] = ps
+            if br == 3:
+                zc = (i // 4) * D + 512 + (i % 4) * P
+                nc.tensor.matmul(
+                    out=ps[:], lhsT=zuT[:, zc : zc + P], rhs=zuT[:, hf * D : hf * D + 512], start=True, stop=True
+                )
+            else:
+                for g in range(2):
+                    ls = slice(i * 256 + g * P, i * 256 + (g + 1) * P)
                     rs = slice(g * 1024 + hf * 512, g * 1024 + hf * 512 + 512)
                     nc.tensor.matmul_mx(
-                        out=ps[:], lhsT=hq[:, ls].bitcast(FP8X4), lhsT_scale=hs[:, ls],
-                        rhs=cq[:, rs].bitcast(FP8X4), rhs_scale=cs[:, rs],
+                        out=ps[:], lhsT=xq[:, ls].bitcast(FP8X4), lhsT_scale=xs[:, ls],
+                        rhs=u1q[:, rs].bitcast(FP8X4), rhs_scale=u1s[:, rs],
                         start=(g == 0), stop=(g == 1),
                     )
 
-            def add_bias(hf):
-                if ("ot", i) not in live:
-                    live["ot", i] = big.tile([P, D], F32, tag="k4", name="ot%d" % i, align_bytes=64)
-                sl = slice(hf * 512, (hf + 1) * 512)
-                nc.vector.tensor_tensor(
-                    out=live["ot", i][:, sl], in0=live["ps2", i, hf][:], in1=bcc[:, sl], op=ALU.add
+        def unit_add_bias(br, i, hf):
+            if hf == 0:
+                live["n", br, i] = vnp.tile([P, D], F32, name="n%d_%d" % (br, i))
+                live["ssum", br, i] = stat.tile([P, 2], F32, tag="ssum", name="ssum%d_%d" % (br, i))
+            sl = slice(hf * 512, (hf + 1) * 512)
+            nc.vector.scalar_tensor_tensor(
+                out=live["n", br, i][:, sl], in0=live["ps", br, i, hf][:], scalar=1.0, in1=bcs[br][:, sl],
+                op0=ALU.mult, op1=ALU.add, accum_out=live["ssum", br, i][:, hf : hf + 1],
+            )
+
+        def unit_mean(br, i):
+            negmean = stat.tile([P, 1], F32, tag="negmean", name="negmean%d_%d" % (br, i))
+            live["nm", br, i] = negmean
+            ssum = live["ssum", br, i]
+            nc.gpsimd.tensor_scalar(
+                out=negmean[:], in0=ssum[:, 0:1], scalar1=ssum[:, 1:2], scalar2=-1.0 / D, op0=ALU.add, op1=ALU.mult
+            )
+
+        def unit_squares(br, i):
+            junk = junkp.tile([P, D], BF16, tag="junk", name="junk%d_%d" % (br, i))
+            sq = stat.tile([P, 1], F32, tag="sq", name="sq%d_%d" % (br, i))
+            live["sq", br, i] = sq
+            nc.scalar.activation(
+                out=junk[:], in_=live["n", br, i][:], func=ACT.Square, bias=live["nm", br, i][:, 0:1], scale=1.0,
+                accum_out=sq[:, 0:1],
+            )
+
+        def unit_std(br, i):
+            std = stat.tile([P, 1], F32, tag="std", name="std%d_%d" % (br, i))
+            live["std", br, i] = std
+            nc.scalar.activation(out=std[:], in_=live["sq", br, i][:], func=ACT.Sqrt, bias=epsc[:, 0:1], scale=1.0 / D)
+
+        def unit_normalise(br, i):
+            rstd = stat.tile([P, 1], F32, tag="rstd", name="rstd%d_%d" % (br, i))
+            nc.vector.reciprocal(out=rstd[:], in_=live["std", br, i][:])
+            v = live["n", br, i]
+            nc.gpsimd.tensor_scalar(
+                out=v[:], in0=v[:], scalar1=live["nm", br, i][:, 0:1], scalar2=rstd[:, 0:1], op0=ALU.add, op1=ALU.mult
+            )
+
+        def gain_transpose():
+            pv = psum.tile([P, BANK], F32, tag="bank", name="pv")
+            live["pv"] = pv
+            nc.tensor.transpose(out=pv[:, 0:P], in_=vrows[:], identity=identF[:])
+
+        def gain_columns():
+            vw = const.tile([P, 16], F32, name="vw")
+            nc.vector.tensor_copy(out=vw[:], in_=live["pv"][:, 0:16])
+            nc.vector.tensor_copy(out=cols[:], in_=vw[:].bitcast(BF16))
+            al = const.tile([P, 1], F32, name="al")
+            nc.vector.tensor_copy(out=al[:], in_=al_bf[:])
+            nc.vector.tensor_scalar(out=g3p[:], in0=cols[:, 16:24], scalar1=al[:, 0:1], scalar2=None, op0=ALU.mult)
+            nc.vector.tensor_scalar(
+                out=b3p[:], in0=cols[:, 24:32], scalar1=al[:, 0:1], scalar2=1.0, op0=ALU.mult, op1=ALU.add
+            )
+
+        def block_transposes(br, i0, jt):
+            bank = psum.tile([P, BANK], F32, tag="bank", name="nb%d_%d_%d" % (br, i0, jt))
+            live["nb", br, i0, jt] = bank
+            for il in range(2):
+                nc.tensor.transpose(
+                    out=bank[:, il * P : (il + 1) * P],
+                    in_=live["n", br, i0 + il][:, jt * P : (jt + 1) * P],
+                    identity=identF[:],
                 )
 
-            def store():
-                nc.sync.dma_start(out=o_v[:, i, :], in_=live["ot", i][:])
+        def block_affine(br, i0, jt, on_vector):
+            (g, t) = (jt // 4, jt % 4)
+            if t == 0:
+                live["o", br, i0, g] = big.tile(
+                    [P, 4, 2 * P], F32, tag="k4", name="o%d_%d_%d" % (br, i0, g), align_bytes=64
+                )
+            gcol = cols[:, jt : jt + 1] if br == 1 else g3p[:, jt : jt + 1]
+            bcol = cols[:, 8 + jt : 9 + jt] if br == 1 else b3p[:, jt : jt + 1]
+            dst = live["o", br, i0, g][:, t, :]
+            src = live["nb", br, i0, jt][:, 0 : 2 * P]
+            if on_vector:
+                nc.vector.tensor_scalar(out=dst, in0=src, scalar1=gcol, scalar2=bcol, op0=ALU.mult, op1=ALU.add)
+            else:
+                nc.scalar.activation(out=dst, in_=src, func=ACT.Identity, bias=bcol, scale=gcol)
 
-            def store_half(hf):
-                sl = slice(hf * 512, (hf + 1) * 512)
-                nc.sync.dma_start(out=o_v[:, i, sl], in_=live["ot", i][:, sl])
+        def gate(i0, g):
+            hg = grp.tile([P, 8 * P], BF16, tag="hg", name="hg%d_%d" % (i0, g), align_bytes=64)
+            live["hg", i0, g] = hg
+            nc.vector.tensor_tensor(
+                out=hg[:].rearrange("p (c i t) -> p c t i", i=4, t=4),
+                in0=live["o", 1, i0, g][:].rearrange("p t (c i) -> p c t i", i=4),
+                in1=live["o", 3, i0, g][:].rearrange("p t (c i) -> p c t i", i=4),
+                op=ALU.mult,
+            )
 
-            for hf in range(2):
-                ops["s.pe", i, hf] = lambda hf=hf: pe(hf)
-                ops["s.add", i, hf] = lambda hf=hf: add_bias(hf)
-            ops["s.st", i] = store
-            for hf in range(2):
-                ops["s.sth", i, hf] = lambda hf=hf: store_half(hf)
+        def quantise_h(i0, g):
+            sl = slice(g * 1024 + i0 * P, g * 1024 + (i0 + 2) * P)
+            nc.vector.quantize_mx(out=hq[:, sl].bitcast(FP8X4), scales=hs[:, sl], in_=live["hg", i0, g][:])
 
-        for k in range(2):
-            unit_zu(k)
-        for br in (3, 1):
-            unit_bc(br)
-            for i in range(NT):
-                unit_a(br, i, NORM_ENGINE.get((br, i), "pool"))
-        for w in ("U", "C"):
-            for jt in range(8):
-                unit_w(w, jt, "dve" if (w, jt) in EVD else "act")
-            for hf in range(2):
-                unit_wq(w, hf)
-        for i in range(NT):
-            unit_x(i, "dve" if ("X", i) in EVD else "act")
-            unit_s(i)
-        for c in range(4):
-            unit_xq(c)
-        unit_cols()
-        for (k, (i0, ntl)) in enumerate(GROUPS):
+        def stage2_matmul(i, hf):
+            ps = psum.tile([P, BANK], F32, tag="bank", name="ps2_%d_%d" % (i, hf))
+            live["ps2", i, hf] = ps
             for g in range(2):
-                for t in range(4):
-                    unit_b(i0, ntl, g, t, "dve" if t >= 4 - NDVE[2 * k + g] else "act")
-                unit_f(i0, ntl, g, "pool" if GPOOL[2 * k + g] else "dve")
-        for name in plan():
-            ops[name]()
+                ls = slice(g * 1024 + i * P, g * 1024 + (i + 1) * P)
+                rs = slice(g * 1024 + hf * 512, g * 1024 + hf * 512 + 512)
+                nc.tensor.matmul_mx(
+                    out=ps[:], lhsT=hq[:, ls].bitcast(FP8X4), lhsT_scale=hs[:, ls],
+                    rhs=cq[:, rs].bitcast(FP8X4), rhs_scale=cs[:, rs],
+                    start=(g == 0), stop=(g == 1),
+                )
+
+        def stage2_finish(i, hf):
+            if hf == 0:
+                live["ot", i] = big.tile([P, D], F32, tag="k4", name="ot%d" % i, align_bytes=64)
+            sl = slice(hf * 512, (hf + 1) * 512)
+            nc.vector.tensor_tensor(out=live["ot", i][:, sl], in0=live["ps2", i, hf][:], in1=bcc[:, sl], op=ALU.add)
+            nc.sync.dma_start(out=o_v[:, i, sl], in_=live["ot", i][:, sl])
+
+        def slot(s):
+            for (kind, j) in word_banks_of_slot(s + 1):
+                word_transposes(kind, j)
+            if s == SLOT_BIAS1:
+                plane_matmul(1, 0)
+                plane_matmul(1, 1)
+                gain_transpose()
+            if s > 0:
+                for (br, i) in units_of_slot(s):
+                    unit_matmul(br, i, 0)
+                    unit_matmul(br, i, 1)
+            for (br, i) in units_of_slot(s - LAG_MEAN):
+                unit_mean(br, i)
+            for (br, i) in units_of_slot(s - LAG_NORMALISE):
+                unit_normalise(br, i)
+            if s == SLOT_BIAS1:
+                plane_copy(1, 0)
+                plane_copy(1, 1)
+                gain_columns()
+            for (br, i) in units_of_slot(s):
+                unit_add_bias(br, i, 0)
+                unit_add_bias(br, i, 1)
+            for (kind, j) in word_banks_of_slot(s - 1):
+                quantise_if_complete(kind, j)
+            mine = word_banks_of_slot(s)
+            for (kind, j) in mine[:1]:
+                word_copy(kind, j)
+            for (br, i) in units_of_slot(s - LAG_SQUARES):
+                unit_squares(br, i)
+            for (kind, j) in mine[1:]:
+                word_copy(kind, j)
+            for (br, i) in units_of_slot(s - LAG_SQUARES):
+                unit_std(br, i)
+
+        def cycle(c):
+            blocks = [(br, 2 * (c // 2), 4 * (c % 2) + t) for t in range(4) for br in (3, 1)] if c < N_CYCLES else []
+            tiles = [c - LAG_STAGE2] if 0 <= c - LAG_STAGE2 < NT else []
+            gates = [(2 * ((c - 1) // 2), (c - 1) % 2)] if 1 <= c <= N_CYCLES else []
+            for (br, i0, jt) in blocks:
+                block_transposes(br, i0, jt)
+            for i in tiles:
+                stage2_matmul(i, 0)
+                stage2_matmul(i, 1)
+            for (br, i0, jt) in blocks:
+                block_affine(br, i0, jt, c == CYCLE_ON_VECTOR)
+            for (i0, g) in gates:
+                gate(i0, g)
+            for i in tiles:
+                stage2_finish(i, 0)
+            for (i0, g) in gates:
+                quantise_h(i0, g)
+            for i in tiles:
+                stage2_finish(i, 1)
+
+        small_transposes(0)
+        plane_matmul(3, 0)
+        plane_matmul(3, 1)
+        small_transposes(1)
+        small_copy(0)
+        plane_copy(3, 0)
+        plane_copy(3, 1)
+        small_copy(1)
+        unit_matmul(3, 0, 0)
+        for (kind, j) in word_banks_of_slot(0):
+            word_transposes(kind, j)
+        unit_matmul(3, 0, 1)
+        n_slots = len(UNITS) + LAG_NORMALISE + 1
+        for s in range(n_slots):
+            slot(s)
+            if s >= FIRST_CYCLE_SLOT:
+                cycle(s - FIRST_CYCLE_SLOT)
+        for c in range(n_slots - FIRST_CYCLE_SLOT, N_CYCLES + LAG_STAGE2):
+            cycle(c)

from contextlib import ExitStack

import concourse.mybir as mybir
from concourse.masks import make_identity

F32 = mybir.dt.float32
BF16 = mybir.dt.bfloat16
U32 = mybir.dt.uint32
U8 = mybir.dt.uint8
FP8X4 = mybir.dt.float8_e4m3fn_x4
ALU = mybir.AluOpType
ACT = mybir.ActivationFunctionType

P = 128
NT = 8
D = 1024
BANK = 512
EPS = 1e-6
FLOPS = 2 * 1024 * (1024 * 1024 * 2 + 128 * 1024)

UNITS = tuple([(3, i) for i in range(NT)] + [(1, i) for i in range(NT)])
WORD_BANKS = tuple([("U", j) for j in range(8)] + [("x", i) for i in range(NT)] + [("C", j) for j in range(8)])
SLOTS_4K = 20

LAG_MEAN = 1
LAG_SQUARES = 3
LAG_NORMALISE = 4
FAST_SLOTS = 10
SLOT_BIAS1 = 5
N_CYCLES = 8
LAG_STAGE2 = 3
FIRST_CYCLE_SLOT = 15
CYCLE_ON_VECTOR = 1


def word_banks_of_slot(s):
    def upto(n):
        return min(len(WORD_BANKS), 2 * n if n <= FAST_SLOTS else FAST_SLOTS + n)

    return WORD_BANKS[upto(s) : upto(s + 1)] if s >= 0 else ()


def units_of_slot(s):
    return UNITS[s : s + 1] if s >= 0 else ()


def tile_polymlp_skiplora_pa_kernel(
    tc, x, z2, U1_w, U1_b, U3_w, U3_b, C_w, C_b, ln1_g, ln1_b, ln3_g, ln3_b, alpha, out
):
    nc = tc.nc
    with ExitStack() as ctx:
        const = ctx.enter_context(tc.tile_pool(name="const", bufs=1))
        big = ctx.enter_context(tc.tile_pool(name="big", bufs=SLOTS_4K))
        browp = ctx.enter_context(tc.tile_pool(name="browp", bufs=2))
        grp = ctx.enter_context(tc.tile_pool(name="grp", bufs=2))
        vnp = ctx.enter_context(tc.tile_pool(name="vnp", bufs=1))
        stat = ctx.enter_context(tc.tile_pool(name="stat", bufs=8))
        junkp = ctx.enter_context(tc.tile_pool(name="junkp", bufs=1))
        psum = ctx.enter_context(tc.psum_pool(name="psum", bufs=8))

        xf = x.flatten_outer_dims()
        zf = z2.flatten_outer_dims()
        of = out.flatten_outer_dims()
        x_v = xf.rearrange("(p c j) d -> c p (j d)", c=4, j=2)
        z_v = zf.rearrange("(p i) q -> p (i q)", i=NT)
        o_v = of.rearrange("(p i) d -> p i d", i=NT)
        u1_v = U1_w.rearrange("(a p e) d -> a p (e d)", a=4, e=2)
        u3_v = U3_w.rearrange("(a p e) q -> p a (e q)", a=4, e=2)
        c_v = C_w.rearrange("(c j p) h -> c p j h", c=4, j=2)

        u3raw = const.tile([P, D], BF16)
        z2raw = const.tile([P, D], BF16)
        for k in range(2):
            nc.sync.dma_start(
                out=u3raw[:, k * 512 : (k + 1) * 512].rearrange("p (a w) -> p a w", a=2),
                in_=u3_v[:, 2 * k : 2 * k + 2, :],
            )
            nc.sync.dma_start(out=z2raw[:, k * 512 : (k + 1) * 512], in_=z_v[:, k * 512 : (k + 1) * 512])

        identB = const.tile([P, P], BF16)
        make_identity(nc, identB[:])
        identF = const.tile([P, P], F32)
        make_identity(nc, identF[:])
        ones = const.tile([P, P], BF16)
        nc.vector.memset(ones[:], 1.0)

        def bias_row(vec, nm):
            brow = browp.tile([P, D], BF16, tag="brow", name=nm)
            nc.vector.memset(brow[:], 0.0)
            nc.sync.dma_start(out=brow[0:1, :], in_=vec.rearrange("(o n) -> o n", o=1))
            return brow

        def load_raw(src, nm, split):
            t = big.tile([P, 2 * D], BF16, tag="k4", name=nm, align_bytes=64)
            if split:
                nc.sync.dma_start(out=t[:].rearrange("p (j h) -> p j h", j=2), in_=src)
            else:
                nc.sync.dma_start(out=t[:], in_=src)
            return t

        brows = {3: bias_row(U3_b, "brow3")}
        epsc = const.tile([P, 1], F32)
        nc.vector.memset(epsc[:], EPS)
        warm = const.tile([P, 1], F32)
        nc.scalar.activation(out=warm[:], in_=epsc[:], func=ACT.Sqrt)
        vrows = const.tile([P, P], F32)
        nc.vector.memset(vrows[:], 0.0)
        u1raw = [load_raw(u1_v[a], "u1raw%d" % a, False) for a in range(4)]
        brows[1] = bias_row(U1_b, "brow1")
        xraw = [load_raw(x_v[c], "xraw%d" % c, False) for c in range(4)]
        for v, vec in enumerate((ln1_g, ln1_b, ln3_g, ln3_b)):
            nc.sync.dma_start(
                out=vrows[4 * v : 4 * v + 4, :].bitcast(BF16), in_=vec.rearrange("(r w) -> r w", r=4)
            )
        al_bf = const.tile([P, 1], BF16)
        nc.sync.dma_start(out=al_bf[:], in_=alpha.partition_broadcast(P))
        craw = [load_raw(c_v[c], "craw%d" % c, True) for c in range(4)]
        bcc = const.tile([P, D], BF16)
        nc.sync.dma_start(out=bcc[:], in_=C_b.partition_broadcast(P))

        xq = const.tile([P, 2048], U32, align_bytes=64)
        xs = const.tile([P, 2048], U8, align_bytes=64)
        u1q = const.tile([P, 2048], U32, align_bytes=64)
        u1s = const.tile([P, 2048], U8, align_bytes=64)
        cq = const.tile([P, 2048], U32, align_bytes=64)
        cs = const.tile([P, 2048], U8, align_bytes=64)
        hq = const.tile([P, 2048], U32, align_bytes=64)
        hs = const.tile([P, 2048], U8, align_bytes=64)
        zuT = const.tile([P, 2048], BF16)
        bcs = {1: const.tile([P, D], F32, name="bc1"), 3: const.tile([P, D], F32, name="bc3")}
        cols = const.tile([P, 32], F32)
        g3p = const.tile([P, 8], F32)
        b3p = const.tile([P, 8], F32)
        raws = {"U": u1raw, "x": xraw, "C": craw}
        packed = {"U": (u1q, u1s), "C": (cq, cs)}

        live = {}

        def small_transposes(k):
            pb = psum.tile([P, D], BF16, tag="bank", name="pb%d" % k)
            live["pb", k] = pb
            for m in range(8):
                raw = u3raw if m < 4 else z2raw
                col = (4 * k + m % 4) * P
                nc.tensor.transpose(out=pb[:, m * P : (m + 1) * P], in_=raw[:, col : col + P], identity=identB[:])

        def small_copy(k):
            nc.scalar.copy(out=zuT[:, k * D : (k + 1) * D], in_=live["pb", k][:])

        def plane_matmul(br, hf):
            ps = psum.tile([P, BANK], F32, tag="bank", name="bps%d%d" % (br, hf))
            live["bps", br, hf] = ps
            nc.tensor.matmul(
                out=ps[:], lhsT=ones[:], rhs=brows[br][:, hf * 512 : (hf + 1) * 512], start=True, stop=True
            )

        def plane_copy(br, hf):
            nc.vector.tensor_copy(
                out=bcs[br][:, hf * 512 : (hf + 1) * 512].rearrange("p (a e r) -> p a e r", a=2, e=2),
                in_=live["bps", br, hf][:].rearrange("p (a r e) -> p a e r", a=2, e=2),
            )

        def word_transposes(kind, j):
            bank = psum.tile([P, BANK], F32, tag="bank", name="wb%s%d" % (kind, j))
            live["wb", kind, j] = bank
            words = raws[kind][j // 2][:].bitcast(F32)
            for c in range(4):
                nc.tensor.transpose(
                    out=bank[:, c * P : (c + 1) * P],
                    in_=words[:, (j % 2) * 512 + c * P : (j % 2) * 512 + (c + 1) * P],
                    identity=identF[:],
                )

        def word_copy(kind, j):
            src = live["wb", kind, j][:].rearrange("p (g u r) -> p g r u", g=2, u=2)
            if kind == "x":
                if j % 2 == 0:
                    live["xg", j // 2] = big.tile([P, 2048], BF16, tag="k4", name="xg%d" % (j // 2), align_bytes=64)
                view = live["xg", j // 2][:].bitcast(F32).rearrange("p (j g r u) -> p j g r u", j=2, g=2, u=2)
                nc.scalar.copy(out=view[:, j % 2, :, :, :], in_=src)
            else:
                if j % 4 == 0:
                    live["wg", kind, j // 4] = grp.tile(
                        [P, 4096], BF16, tag="wg", name="wg%s%d" % (kind, j // 4), align_bytes=64
                    )
                view = live["wg", kind, j // 4][:].bitcast(F32).rearrange("p (g j r u) -> p g j r u", g=2, j=4, u=2)
                nc.scalar.copy(out=view[:, :, j % 4, :, :], in_=src)

        def quantise_if_complete(kind, j):
            if kind == "x" and j % 2 == 1:
                sl = slice((j // 2) * 512, (j // 2 + 1) * 512)
                nc.vector.quantize_mx(out=xq[:, sl].bitcast(FP8X4), scales=xs[:, sl], in_=live["xg", j // 2][:])
            if kind != "x" and j % 4 == 3:
                (codes, scales) = packed[kind]
                for g in range(2):
                    sl = slice(g * 1024 + (j // 4) * 512, g * 1024 + (j // 4) * 512 + 512)
                    nc.vector.quantize_mx(
                        out=codes[:, sl].bitcast(FP8X4), scales=scales[:, sl],
                        in_=live["wg", kind, j // 4][:, g * 2048 : (g + 1) * 2048],
                    )

        def unit_matmul(br, i, hf):
            ps = psum.tile([P, BANK], F32, tag="bank", name="ps%d_%d_%d" % (br, i, hf))
            live["ps", br, i, hf] = ps
            if br == 3:
                zc = (i // 4) * D + 512 + (i % 4) * P
                nc.tensor.matmul(
                    out=ps[:], lhsT=zuT[:, zc : zc + P], rhs=zuT[:, hf * D : hf * D + 512], start=True, stop=True
                )
            else:
                for g in range(2):
                    ls = slice(i * 256 + g * P, i * 256 + (g + 1) * P)
                    rs = slice(g * 1024 + hf * 512, g * 1024 + hf * 512 + 512)
                    nc.tensor.matmul_mx(
                        out=ps[:], lhsT=xq[:, ls].bitcast(FP8X4), lhsT_scale=xs[:, ls],
                        rhs=u1q[:, rs].bitcast(FP8X4), rhs_scale=u1s[:, rs],
                        start=(g == 0), stop=(g == 1),
                    )

        def unit_add_bias(br, i, hf):
            if hf == 0:
                live["n", br, i] = vnp.tile([P, D], F32, name="n%d_%d" % (br, i))
                live["ssum", br, i] = stat.tile([P, 2], F32, tag="ssum", name="ssum%d_%d" % (br, i))
            sl = slice(hf * 512, (hf + 1) * 512)
            nc.vector.scalar_tensor_tensor(
                out=live["n", br, i][:, sl], in0=live["ps", br, i, hf][:], scalar=1.0, in1=bcs[br][:, sl],
                op0=ALU.mult, op1=ALU.add, accum_out=live["ssum", br, i][:, hf : hf + 1],
            )

        def unit_mean(br, i):
            negmean = stat.tile([P, 1], F32, tag="negmean", name="negmean%d_%d" % (br, i))
            live["nm", br, i] = negmean
            ssum = live["ssum", br, i]
            nc.gpsimd.tensor_scalar(
                out=negmean[:], in0=ssum[:, 0:1], scalar1=ssum[:, 1:2], scalar2=-1.0 / D, op0=ALU.add, op1=ALU.mult
            )

        def unit_squares(br, i):
            junk = junkp.tile([P, D], BF16, tag="junk", name="junk%d_%d" % (br, i))
            sq = stat.tile([P, 1], F32, tag="sq", name="sq%d_%d" % (br, i))
            live["sq", br, i] = sq
            nc.scalar.activation(
                out=junk[:], in_=live["n", br, i][:], func=ACT.Square, bias=live["nm", br, i][:, 0:1], scale=1.0,
                accum_out=sq[:, 0:1],
            )

        def unit_std(br, i):
            std = stat.tile([P, 1], F32, tag="std", name="std%d_%d" % (br, i))
            live["std", br, i] = std
            nc.scalar.activation(out=std[:], in_=live["sq", br, i][:], func=ACT.Sqrt, bias=epsc[:, 0:1], scale=1.0 / D)

        def unit_normalise(br, i):
            rstd = stat.tile([P, 1], F32, tag="rstd", name="rstd%d_%d" % (br, i))
            nc.vector.reciprocal(out=rstd[:], in_=live["std", br, i][:])
            v = live["n", br, i]
            nc.gpsimd.tensor_scalar(
                out=v[:], in0=v[:], scalar1=live["nm", br, i][:, 0:1], scalar2=rstd[:, 0:1], op0=ALU.add, op1=ALU.mult
            )

        def gain_transpose():
            pv = psum.tile([P, BANK], F32, tag="bank", name="pv")
            live["pv"] = pv
            nc.tensor.transpose(out=pv[:, 0:P], in_=vrows[:], identity=identF[:])

        def gain_columns():
            vw = const.tile([P, 16], F32, name="vw")
            nc.vector.tensor_copy(out=vw[:], in_=live["pv"][:, 0:16])
            nc.vector.tensor_copy(out=cols[:], in_=vw[:].bitcast(BF16))
            al = const.tile([P, 1], F32, name="al")
            nc.vector.tensor_copy(out=al[:], in_=al_bf[:])
            nc.vector.tensor_scalar(out=g3p[:], in0=cols[:, 16:24], scalar1=al[:, 0:1], scalar2=None, op0=ALU.mult)
            nc.vector.tensor_scalar(
                out=b3p[:], in0=cols[:, 24:32], scalar1=al[:, 0:1], scalar2=1.0, op0=ALU.mult, op1=ALU.add
            )

        def block_transposes(br, i0, jt):
            bank = psum.tile([P, BANK], F32, tag="bank", name="nb%d_%d_%d" % (br, i0, jt))
            live["nb", br, i0, jt] = bank
            for il in range(2):
                nc.tensor.transpose(
                    out=bank[:, il * P : (il + 1) * P],
                    in_=live["n", br, i0 + il][:, jt * P : (jt + 1) * P],
                    identity=identF[:],
                )

        def block_affine(br, i0, jt, on_vector):
            (g, t) = (jt // 4, jt % 4)
            if t == 0:
                live["o", br, i0, g] = big.tile(
                    [P, 4, 2 * P], F32, tag="k4", name="o%d_%d_%d" % (br, i0, g), align_bytes=64
                )
            gcol = cols[:, jt : jt + 1] if br == 1 else g3p[:, jt : jt + 1]
            bcol = cols[:, 8 + jt : 9 + jt] if br == 1 else b3p[:, jt : jt + 1]
            dst = live["o", br, i0, g][:, t, :]
            src = live["nb", br, i0, jt][:, 0 : 2 * P]
            if on_vector:
                nc.vector.tensor_scalar(out=dst, in0=src, scalar1=gcol, scalar2=bcol, op0=ALU.mult, op1=ALU.add)
            else:
                nc.scalar.activation(out=dst, in_=src, func=ACT.Identity, bias=bcol, scale=gcol)

        def gate(i0, g):
            hg = grp.tile([P, 8 * P], BF16, tag="hg", name="hg%d_%d" % (i0, g), align_bytes=64)
            live["hg", i0, g] = hg
            nc.vector.tensor_tensor(
                out=hg[:].rearrange("p (c i t) -> p c t i", i=4, t=4),
                in0=live["o", 1, i0, g][:].rearrange("p t (c i) -> p c t i", i=4),
                in1=live["o", 3, i0, g][:].rearrange("p t (c i) -> p c t i", i=4),
                op=ALU.mult,
            )

        def quantise_h(i0, g):
            sl = slice(g * 1024 + i0 * P, g * 1024 + (i0 + 2) * P)
            nc.vector.quantize_mx(out=hq[:, sl].bitcast(FP8X4), scales=hs[:, sl], in_=live["hg", i0, g][:])

        def stage2_matmul(i, hf):
            ps = psum.tile([P, BANK], F32, tag="bank", name="ps2_%d_%d" % (i, hf))
            live["ps2", i, hf] = ps
            for g in range(2):
                ls = slice(g * 1024 + i * P, g * 1024 + (i + 1) * P)
                rs = slice(g * 1024 + hf * 512, g * 1024 + hf * 512 + 512)
                nc.tensor.matmul_mx(
                    out=ps[:], lhsT=hq[:, ls].bitcast(FP8X4), lhsT_scale=hs[:, ls],
                    rhs=cq[:, rs].bitcast(FP8X4), rhs_scale=cs[:, rs],
                    start=(g == 0), stop=(g == 1),
                )

        def stage2_finish(i, hf):
            if hf == 0:
                live["ot", i] = big.tile([P, D], F32, tag="k4", name="ot%d" % i, align_bytes=64)
            sl = slice(hf * 512, (hf + 1) * 512)
            nc.vector.tensor_tensor(out=live["ot", i][:, sl], in0=live["ps2", i, hf][:], in1=bcc[:, sl], op=ALU.add)
            nc.sync.dma_start(out=o_v[:, i, sl], in_=live["ot", i][:, sl])

        def slot(s):
            for (kind, j) in word_banks_of_slot(s + 1):
                word_transposes(kind, j)
            if s == SLOT_BIAS1:
                plane_matmul(1, 0)
                plane_matmul(1, 1)
                gain_transpose()
            if s > 0:
                for (br, i) in units_of_slot(s):
                    unit_matmul(br, i, 0)
                    unit_matmul(br, i, 1)
            for (br, i) in units_of_slot(s - LAG_MEAN):
                unit_mean(br, i)
            for (br, i) in units_of_slot(s - LAG_NORMALISE):
                unit_normalise(br, i)
            if s == SLOT_BIAS1:
                plane_copy(1, 0)
                plane_copy(1, 1)
                gain_columns()
            for (br, i) in units_of_slot(s):
                unit_add_bias(br, i, 0)
                unit_add_bias(br, i, 1)
            for (kind, j) in word_banks_of_slot(s - 1):
                quantise_if_complete(kind, j)
            mine = word_banks_of_slot(s)
            for (kind, j) in mine[:1]:
                word_copy(kind, j)
            for (br, i) in units_of_slot(s - LAG_SQUARES):
                unit_squares(br, i)
            for (kind, j) in mine[1:]:
                word_copy(kind, j)
            for (br, i) in units_of_slot(s - LAG_SQUARES):
                unit_std(br, i)

        def cycle(c):
            blocks = [(br, 2 * (c // 2), 4 * (c % 2) + t) for t in range(4) for br in (3, 1)] if c < N_CYCLES else []
            tiles = [c - LAG_STAGE2] if 0 <= c - LAG_STAGE2 < NT else []
            gates = [(2 * ((c - 1) // 2), (c - 1) % 2)] if 1 <= c <= N_CYCLES else []
            for (br, i0, jt) in blocks:
                block_transposes(br, i0, jt)
            for i in tiles:
                stage2_matmul(i, 0)
                stage2_matmul(i, 1)
            for (br, i0, jt) in blocks:
                block_affine(br, i0, jt, c == CYCLE_ON_VECTOR)
            for (i0, g) in gates:
                gate(i0, g)
            for i in tiles:
                stage2_finish(i, 0)
            for (i0, g) in gates:
                quantise_h(i0, g)
            for i in tiles:
                stage2_finish(i, 1)

        small_transposes(0)
        plane_matmul(3, 0)
        plane_matmul(3, 1)
        small_transposes(1)
        small_copy(0)
        plane_copy(3, 0)
        plane_copy(3, 1)
        small_copy(1)
        unit_matmul(3, 0, 0)
        for (kind, j) in word_banks_of_slot(0):
            word_transposes(kind, j)
        unit_matmul(3, 0, 1)
        n_slots = len(UNITS) + LAG_NORMALISE + 1
        for s in range(n_slots):
            slot(s)
            if s >= FIRST_CYCLE_SLOT:
                cycle(s - FIRST_CYCLE_SLOT)
        for c in range(n_slots - FIRST_CYCLE_SLOT, N_CYCLES + LAG_STAGE2):
            cycle(c)
